import numpy as np
import ml_dtypes


def mxq(x, axis, fmt="e4m3"):
    dtype, down = {"e4m3": (ml_dtypes.float8_e4m3fn, 7), "e5m2": (ml_dtypes.float8_e5m2, 14)}[fmt]
    v = np.moveaxis(np.asarray(x, np.float32).astype(ml_dtypes.bfloat16).astype(np.float64), axis, -1)
    blocks = v.reshape(v.shape[:-1] + (-1, 32))
    amax = np.abs(blocks).max(-1, keepdims=True)
    byte = np.maximum(np.where(amax > 0, np.frexp(amax)[1] - 1 + 127, 0) - down, 1)
    scale = np.exp2(byte - 127.0)
    codes = (blocks / scale).astype(np.float32).astype(dtype).astype(np.float64)
    return np.moveaxis((codes * scale).reshape(v.shape), -1, axis)


WIDE = False


def mx_kscale(k):
    if not WIDE:
        return np.ones(k)
    levels = np.array([10, -10, 5, -5, 0])
    a = np.random.permutation(np.resize(levels, k // 512 * 4)).reshape(k // 512, 4)
    idx = np.arange(k)
    return np.exp2(a[idx // 512, idx % 128 // 32])


BF16 = ml_dtypes.bfloat16


def bf(x):
    return np.asarray(x, np.float32).astype(BF16)


def f64(x):
    return np.asarray(x).astype(np.float64)


B, N, F, T, DE, FO, K = 8, 1024, 16, 8, 16, 32, 3
C = F * T


def setup_inputs():
    s = mx_kscale(N)
    return {"supports": bf(np.abs(np.random.standard_normal((N, N))) * 0.4 / np.sqrt(N)),
            "cheb_2": bf(np.random.standard_normal((N, N)) * 0.8 / np.sqrt(N)),
            "spatial_attention": bf(np.random.random((B, N, N)) * s[None, :, None]),
            "x": bf(np.random.standard_normal((B, N, F, T)) / s[None, :, None, None])}


def reference(supports, cheb_2, spatial_attention, x):
    at = f64(spatial_attention)
    xs = f64(x).reshape(B, N, C)
    xq = mxq(xs, 1, "e4m3")
    r0 = np.diagonal(at, axis1=1, axis2=2)[:, :, None] * xs
    r1 = mxq(f64(supports)[None] * at, 1, "e4m3").transpose(0, 2, 1) @ xq
    r2 = mxq(f64(cheb_2)[None] * at, 1, "e4m3").transpose(0, 2, 1) @ xq
    return np.stack([r0, r1, r2]).reshape(K, B, N, F, T)

@@ -1,0 +1,183 @@
+from contextlib import ExitStack
+
+import concourse.mybir as mybir
+
+BF16 = mybir.dt.bfloat16
+F32 = mybir.dt.float32
+U32 = mybir.dt.uint32
+U8 = mybir.dt.uint8
+FP8X4 = mybir.dt.float8_e4m3fn_x4
+
+P = 128
+PACK = 4
+K_PASS = P * PACK
+
+BATCH = 8
+NODES = 1024
+CHANNELS = 128
+TERMS = 2
+PASSES = NODES // K_PASS
+GROUPED = NODES * PACK
+RUN = 4
+M_TILES_PER_BANK = 4
+BANKS = NODES // (P * M_TILES_PER_BANK)
+X_HALF = BATCH // 2
+DIAG_SLOT = 16
+
+FLOPS = 2 * TERMS * BATCH * NODES * NODES * CHANNELS
+
+
+def interleave(copy, grouped, rows):
+    copy(
+        out=grouped.rearrange("p (c i j) -> p c j i", i=RUN, j=PACK),
+        in_=rows.rearrange("p j (c i) -> p c j i", i=RUN),
+    )
+
+
+def tile_napl_conv_withsat_pb_t_kernel(tc, supports, cheb_2, spatial_attention, x, out):
+    nc = tc.nc
+    terms = (supports, cheb_2)
+
+    with ExitStack() as ctx:
+        keep = ctx.enter_context(tc.tile_pool(name="keep", bufs=1))
+        rows_pool = ctx.enter_context(tc.tile_pool(name="rows", bufs=5))
+        attention_pool = ctx.enter_context(tc.tile_pool(name="attention", bufs=3))
+        product_pool = ctx.enter_context(tc.tile_pool(name="product", bufs=4))
+        operand_pool = ctx.enter_context(tc.tile_pool(name="operand", bufs=2))
+        result_pool = ctx.enter_context(tc.tile_pool(name="result", bufs=4))
+        psum = ctx.enter_context(tc.psum_pool(name="psum", bufs=6))
+
+        def load_rows(matrix, g):
+            rows = rows_pool.tile([P, PACK, NODES], BF16)
+            nc.sync.dma_start(
+                out=rows[:],
+                in_=matrix[g * K_PASS : (g + 1) * K_PASS, :].rearrange("(p j) m -> p j m", j=PACK),
+            )
+            return rows
+
+        diag_bf16 = keep.tile([P, PASSES * PACK, DIAG_SLOT], BF16)
+        diag = keep.tile([P, PASSES * PACK, BATCH], F32)
+        flat_maps = spatial_attention.rearrange("b n m -> b (n m)")
+
+        def load_diagonals():
+            with nc.allow_non_contiguous_dma(reason="the diagonal has one value in each row"):
+                for s in range(PASSES * PACK):
+                    first = ((s // PACK) * K_PASS + s % PACK) * (NODES + 1)
+                    step = PACK * (NODES + 1)
+                    nc.sync.dma_start(
+                        out=diag_bf16[:, s, 0:BATCH],
+                        in_=flat_maps[:, first : first + (P - 1) * step + 1 : step].rearrange("b p -> p b"),
+                    )
+            nc.vector.tensor_copy(out=diag[:], in_=diag_bf16[:, :, 0:BATCH])
+
+        x_rows = []
+        x_codes = keep.tile([P, BATCH * PASSES * CHANNELS], U32, align_bytes=64)
+        x_scales = keep.tile([P, BATCH * PASSES * CHANNELS], U8, align_bytes=64)
+
+        def prepare_x(half):
+            loaded = keep.tile([P, X_HALF, PASSES * PACK, CHANNELS], BF16, name="x_rows%d" % half)
+            nc.sync.dma_start(
+                out=loaded[:].rearrange("p b (g j) c -> p b g (j c)", g=PASSES),
+                in_=x[half * X_HALF : (half + 1) * X_HALF].rearrange(
+                    "b (g p j) f t -> p b g (j f t)", g=PASSES, j=PACK
+                ),
+            )
+            x_rows.append(loaded)
+            x_grouped = product_pool.tile([P, X_HALF * PASSES, CHANNELS, PACK], BF16, align_bytes=64, tag="product")
+            nc.scalar.copy(
+                out=x_grouped[:],
+                in_=loaded[:].rearrange("p b (g j) c -> p (b g) c j", g=PASSES),
+            )
+            cols = slice(half * GROUPED // PACK, (half + 1) * GROUPED // PACK)
+            nc.vector.quantize_mx(
+                out=x_codes[:, cols].bitcast(FP8X4),
+                scales=x_scales[:, cols],
+                in_=x_grouped[:].rearrange("p s c j -> p (s c j)"),
+            )
+
+        term_grouped = {}
+
+        def prepare_terms(g):
+            for k in range(TERMS):
+                rows = load_rows(terms[k], g)
+                grouped = keep.tile([P, GROUPED], BF16, name="term%d_pass%d" % (k, g))
+                interleave(nc.vector.tensor_copy, grouped[:], rows[:])
+                term_grouped[(k, g)] = grouped
+
+        for b in range(BATCH):
+            w_codes = []
+            w_scales = []
+            for k in range(TERMS):
+                w_codes.append(
+                    operand_pool.tile([P, PASSES, NODES], U32, align_bytes=64, name="w_codes%d" % k)
+                )
+                w_scales.append(
+                    operand_pool.tile([P, PASSES, NODES], U8, align_bytes=64, name="w_scales%d" % k)
+                )
+
+            for g in range(PASSES):
+                rows = load_rows(spatial_attention[b], g)
+                if b == 0:
+                    prepare_terms(g)
+                attention = attention_pool.tile([P, GROUPED], BF16)
+                interleave(nc.scalar.copy, attention[:], rows[:])
+                if b % X_HALF == 0 and g == 0:
+                    prepare_x(b // X_HALF)
+                if b == 0 and g == PASSES - 1:
+                    load_diagonals()
+
+                products = []
+                for k in range(TERMS):
+                    product = product_pool.tile([P, GROUPED], BF16, align_bytes=64, tag="product")
+                    nc.vector.tensor_tensor(
+                        out=product[:],
+                        in0=term_grouped[(k, g)][:],
+                        in1=attention[:],
+                        op=mybir.AluOpType.mult,
+                    )
+                    products.append(product)
+                for k in range(TERMS):
+                    nc.vector.quantize_mx(
+                        out=w_codes[k][:, g, :].bitcast(FP8X4),
+                        scales=w_scales[k][:, g, :],
+                        in_=products[k][:],
+                    )
+
+            for k in range(TERMS):
+                for bank in range(BANKS):
+                    acc = psum.tile([P, M_TILES_PER_BANK, CHANNELS], F32)
+                    for t in range(M_TILES_PER_BANK):
+                        first_m = (bank * M_TILES_PER_BANK + t) * P
+                        m_cols = slice(first_m, first_m + P)
+                        for g in range(PASSES):
+                            first_c = (b * PASSES + g) * CHANNELS
+                            x_cols = slice(first_c, first_c + CHANNELS)
+                            nc.tensor.matmul_mx(
+                                out=acc[:, t, :],
+                                lhsT=w_codes[k][:, g, m_cols].bitcast(FP8X4),
+                                lhsT_scale=w_scales[k][:, g, m_cols],
+                                rhs=x_codes[:, x_cols].bitcast(FP8X4),
+                                rhs_scale=x_scales[:, x_cols],
+                                start=(g == 0),
+                                stop=(g == PASSES - 1),
+                            )
+                    result = result_pool.tile([P, M_TILES_PER_BANK, CHANNELS], F32)
+                    nc.scalar.copy(out=result[:], in_=acc[:])
+                    bank_nodes = slice(bank * M_TILES_PER_BANK * P, (bank + 1) * M_TILES_PER_BANK * P)
+                    nc.sync.dma_start(
+                        out=out[1 + k, b, bank_nodes].rearrange("(t q) f s -> q t (f s)", q=P),
+                        in_=result[:],
+                    )
+
+            scaled_x = result_pool.tile([P, PASSES * PACK, CHANNELS], F32)
+            for s in range(PASSES * PACK):
+                nc.scalar.activation(
+                    out=scaled_x[:, s, :],
+                    in_=x_rows[b // X_HALF][:, b % X_HALF, s, :],
+                    func=mybir.ActivationFunctionType.Copy,
+                    scale=diag[:, s, b : b + 1],
+                )
+            nc.sync.dma_start(
+                out=out[0, b].rearrange("(g p j) f t -> p g (j f t)", g=PASSES, j=PACK),
+                in_=scaled_x[:].rearrange("p (g j) c -> p g (j c)", g=PASSES),
+            )

@@ -21,7 +21,6 @@ GROUPED = NODES * PACK
 RUN = 4
 M_TILES_PER_BANK = 4
 BANKS = NODES // (P * M_TILES_PER_BANK)
-X_HALF = BATCH // 2
 DIAG_SLOT = 16
 
 FLOPS = 2 * TERMS * BATCH * NODES * NODES * CHANNELS
@@ -40,10 +39,11 @@ def tile_napl_conv_withsat_pb_t_kernel(tc, supports, cheb_2, spatial_attention, 
 
     with ExitStack() as ctx:
         keep = ctx.enter_context(tc.tile_pool(name="keep", bufs=1))
-        rows_pool = ctx.enter_context(tc.tile_pool(name="rows", bufs=5))
+        rows_pool = ctx.enter_context(tc.tile_pool(name="rows", bufs=6))
         attention_pool = ctx.enter_context(tc.tile_pool(name="attention", bufs=3))
         product_pool = ctx.enter_context(tc.tile_pool(name="product", bufs=4))
         operand_pool = ctx.enter_context(tc.tile_pool(name="operand", bufs=2))
+        x_pool = ctx.enter_context(tc.tile_pool(name="x", bufs=3))
         result_pool = ctx.enter_context(tc.tile_pool(name="result", bufs=4))
         psum = ctx.enter_context(tc.psum_pool(name="psum", bufs=6))
 
@@ -55,45 +55,37 @@ def tile_napl_conv_withsat_pb_t_kernel(tc, supports, cheb_2, spatial_attention, 
             )
             return rows
 
-        diag_bf16 = keep.tile([P, PASSES * PACK, DIAG_SLOT], BF16)
-        diag = keep.tile([P, PASSES * PACK, BATCH], F32)
-        flat_maps = spatial_attention.rearrange("b n m -> b (n m)")
-
-        def load_diagonals():
-            with nc.allow_non_contiguous_dma(reason="the diagonal has one value in each row"):
-                for s in range(PASSES * PACK):
-                    first = ((s // PACK) * K_PASS + s % PACK) * (NODES + 1)
-                    step = PACK * (NODES + 1)
-                    nc.sync.dma_start(
-                        out=diag_bf16[:, s, 0:BATCH],
-                        in_=flat_maps[:, first : first + (P - 1) * step + 1 : step].rearrange("b p -> p b"),
-                    )
-            nc.vector.tensor_copy(out=diag[:], in_=diag_bf16[:, :, 0:BATCH])
-
-        x_rows = []
-        x_codes = keep.tile([P, BATCH * PASSES * CHANNELS], U32, align_bytes=64)
-        x_scales = keep.tile([P, BATCH * PASSES * CHANNELS], U8, align_bytes=64)
-
-        def prepare_x(half):
-            loaded = keep.tile([P, X_HALF, PASSES * PACK, CHANNELS], BF16, name="x_rows%d" % half)
+        def prepare_x(b):
+            x_rows = x_pool.tile([P, PASSES * PACK, CHANNELS], BF16)
             nc.sync.dma_start(
-                out=loaded[:].rearrange("p b (g j) c -> p b g (j c)", g=PASSES),
-                in_=x[half * X_HALF : (half + 1) * X_HALF].rearrange(
-                    "b (g p j) f t -> p b g (j f t)", g=PASSES, j=PACK
-                ),
+                out=x_rows[:].rearrange("p (g j) c -> p g (j c)", g=PASSES),
+                in_=x[b].rearrange("(g p j) f t -> p g (j f t)", g=PASSES, j=PACK),
             )
-            x_rows.append(loaded)
-            x_grouped = product_pool.tile([P, X_HALF * PASSES, CHANNELS, PACK], BF16, align_bytes=64, tag="product")
-            nc.scalar.copy(
-                out=x_grouped[:],
-                in_=loaded[:].rearrange("p b (g j) c -> p (b g) c j", g=PASSES),
-            )
-            cols = slice(half * GROUPED // PACK, (half + 1) * GROUPED // PACK)
+            x_grouped = x_pool.tile([P, PASSES, CHANNELS * PACK], BF16, align_bytes=64)
+            for g in range(PASSES):
+                interleave(nc.scalar.copy, x_grouped[:, g, :], x_rows[:, g * PACK : (g + 1) * PACK, :])
+            x_codes = x_pool.tile([P, PASSES, CHANNELS], U32, align_bytes=64)
+            x_scales = x_pool.tile([P, PASSES, CHANNELS], U8, align_bytes=64)
             nc.vector.quantize_mx(
-                out=x_codes[:, cols].bitcast(FP8X4),
-                scales=x_scales[:, cols],
-                in_=x_grouped[:].rearrange("p s c j -> p (s c j)"),
+                out=x_codes[:].rearrange("p g c -> p (g c)").bitcast(FP8X4),
+                scales=x_scales[:].rearrange("p g c -> p (g c)"),
+                in_=x_grouped[:].rearrange("p g v -> p (g v)"),
             )
+            diag_bf16 = x_pool.tile([P, PASSES, DIAG_SLOT], BF16)
+            flat_map = spatial_attention[b].rearrange("n m -> (n m)")
+            with nc.allow_non_contiguous_dma(reason="the diagonal has one value in each row"):
+                for g in range(PASSES):
+                    first = g * K_PASS * (NODES + 1)
+                    last = first + (K_PASS - 1) * (NODES + 1)
+                    nc.sync.dma_start(
+                        out=diag_bf16[:, g, 0:PACK],
+                        in_=flat_map[first : last + 1 : NODES + 1].rearrange("(p j) -> p j", j=PACK),
+                    )
+            diag = x_pool.tile([P, PASSES * PACK], F32)
+            nc.scalar.copy(
+                out=diag[:].rearrange("p (g j) -> p g j", g=PASSES), in_=diag_bf16[:, :, 0:PACK]
+            )
+            return x_rows, x_codes, x_scales, diag
 
         term_grouped = {}
 
@@ -121,10 +113,8 @@ def tile_napl_conv_withsat_pb_t_kernel(tc, supports, cheb_2, spatial_attention, 
                     prepare_terms(g)
                 attention = attention_pool.tile([P, GROUPED], BF16)
                 interleave(nc.scalar.copy, attention[:], rows[:])
-                if b % X_HALF == 0 and g == 0:
-                    prepare_x(b // X_HALF)
-                if b == 0 and g == PASSES - 1:
-                    load_diagonals()
+                if g == PASSES - 1:
+                    x_rows, x_codes, x_scales, diag = prepare_x(b)
 
                 products = []
                 for k in range(TERMS):
@@ -150,14 +140,12 @@ def tile_napl_conv_withsat_pb_t_kernel(tc, supports, cheb_2, spatial_attention, 
                         first_m = (bank * M_TILES_PER_BANK + t) * P
                         m_cols = slice(first_m, first_m + P)
                         for g in range(PASSES):
-                            first_c = (b * PASSES + g) * CHANNELS
-                            x_cols = slice(first_c, first_c + CHANNELS)
                             nc.tensor.matmul_mx(
                                 out=acc[:, t, :],
                                 lhsT=w_codes[k][:, g, m_cols].bitcast(FP8X4),
                                 lhsT_scale=w_scales[k][:, g, m_cols],
-                                rhs=x_codes[:, x_cols].bitcast(FP8X4),
-                                rhs_scale=x_scales[:, x_cols],
+                                rhs=x_codes[:, g, :].bitcast(FP8X4),
+                                rhs_scale=x_scales[:, g, :],
                                 start=(g == 0),
                                 stop=(g == PASSES - 1),
                             )
@@ -173,9 +161,9 @@ def tile_napl_conv_withsat_pb_t_kernel(tc, supports, cheb_2, spatial_attention, 
             for s in range(PASSES * PACK):
                 nc.scalar.activation(
                     out=scaled_x[:, s, :],
-                    in_=x_rows[b // X_HALF][:, b % X_HALF, s, :],
+                    in_=x_rows[:, s, :],
                     func=mybir.ActivationFunctionType.Copy,
-                    scale=diag[:, s, b : b + 1],
+                    scale=diag[:, s : s + 1],
                 )
             nc.sync.dma_start(
                 out=out[0, b].rearrange("(g p j) f t -> p g (j f t)", g=PASSES, j=PACK),

@@ -21,6 +21,8 @@ GROUPED = NODES * PACK
 RUN = 4
 M_TILES_PER_BANK = 4
 BANKS = NODES // (P * M_TILES_PER_BANK)
+FIRST_PARTS = 2
+LAST_PARTS = 4
 DIAG_SLOT = 16
 
 FLOPS = 2 * TERMS * BATCH * NODES * NODES * CHANNELS
@@ -47,13 +49,16 @@ def tile_napl_conv_withsat_pb_t_kernel(tc, supports, cheb_2, spatial_attention, 
         result_pool = ctx.enter_context(tc.tile_pool(name="result", bufs=4))
         psum = ctx.enter_context(tc.psum_pool(name="psum", bufs=6))
 
-        def load_rows(matrix, g):
-            rows = rows_pool.tile([P, PACK, NODES], BF16)
-            nc.sync.dma_start(
-                out=rows[:],
-                in_=matrix[g * K_PASS : (g + 1) * K_PASS, :].rearrange("(p j) m -> p j m", j=PACK),
-            )
+        def new_rows(parts):
+            rows = rows_pool.tile([P, parts, PACK, NODES // parts], BF16, tag="rows")
             return rows
+
+        def load_rows(rows, matrix, g, part, parts):
+            cols = slice(part * NODES // parts, (part + 1) * NODES // parts)
+            nc.sync.dma_start(
+                out=rows[:, part, :, :],
+                in_=matrix[g * K_PASS : (g + 1) * K_PASS, cols].rearrange("(p j) m -> p j m", j=PACK),
+            )
 
         def prepare_x(b):
             x_rows = x_pool.tile([P, PASSES * PACK, CHANNELS], BF16)
@@ -71,30 +76,34 @@ def tile_napl_conv_withsat_pb_t_kernel(tc, supports, cheb_2, spatial_attention, 
                 scales=x_scales[:].rearrange("p g c -> p (g c)"),
                 in_=x_grouped[:].rearrange("p g v -> p (g v)"),
             )
-            diag_bf16 = x_pool.tile([P, PASSES, DIAG_SLOT], BF16)
+            diag_bf16 = x_pool.tile([P, PASSES, PACK, DIAG_SLOT], BF16)
             flat_map = spatial_attention[b].rearrange("n m -> (n m)")
             with nc.allow_non_contiguous_dma(reason="the diagonal has one value in each row"):
                 for g in range(PASSES):
                     first = g * K_PASS * (NODES + 1)
                     last = first + (K_PASS - 1) * (NODES + 1)
                     nc.sync.dma_start(
-                        out=diag_bf16[:, g, 0:PACK],
-                        in_=flat_map[first : last + 1 : NODES + 1].rearrange("(p j) -> p j", j=PACK),
+                        out=diag_bf16[:, g, :, 0:1],
+                        in_=flat_map[first : last + 1 : NODES + 1].rearrange(
+                            "(p j o) -> p j o", j=PACK, o=1
+                        ),
                     )
             diag = x_pool.tile([P, PASSES * PACK], F32)
             nc.scalar.copy(
-                out=diag[:].rearrange("p (g j) -> p g j", g=PASSES), in_=diag_bf16[:, :, 0:PACK]
+                out=diag[:].rearrange("p (g j) -> p g j", g=PASSES), in_=diag_bf16[:, :, :, 0]
             )
             return x_rows, x_codes, x_scales, diag
 
         term_grouped = {}
 
-        def prepare_terms(g):
-            for k in range(TERMS):
-                rows = load_rows(terms[k], g)
-                grouped = keep.tile([P, GROUPED], BF16, name="term%d_pass%d" % (k, g))
-                interleave(nc.vector.tensor_copy, grouped[:], rows[:])
-                term_grouped[(k, g)] = grouped
+        term_rows = {}
+
+        def parts_of(b, g):
+            if (b, g) == (0, 0):
+                return FIRST_PARTS
+            if (b, g) == (BATCH - 1, PASSES - 1):
+                return LAST_PARTS
+            return 1
 
         for b in range(BATCH):
             w_codes = []
@@ -108,30 +117,50 @@ def tile_napl_conv_withsat_pb_t_kernel(tc, supports, cheb_2, spatial_attention, 
                 )
 
             for g in range(PASSES):
-                rows = load_rows(spatial_attention[b], g)
+                parts = parts_of(b, g)
+                width = GROUPED // parts
+                rows = new_rows(parts)
                 if b == 0:
-                    prepare_terms(g)
-                attention = attention_pool.tile([P, GROUPED], BF16)
-                interleave(nc.scalar.copy, attention[:], rows[:])
-                if g == PASSES - 1:
-                    x_rows, x_codes, x_scales, diag = prepare_x(b)
+                    for k in range(TERMS):
+                        term_rows[k] = new_rows(parts)
+                        grouped = keep.tile([P, GROUPED], BF16, name="term%d_pass%d" % (k, g))
+                        term_grouped[(k, g)] = grouped
+                for part in range(parts):
+                    if b == 0:
+                        for k in range(TERMS):
+                            load_rows(term_rows[k], terms[k], g, part, parts)
+                    load_rows(rows, spatial_attention[b], g, part, parts)
+                for part in range(parts):
+                    span = slice(part * width, (part + 1) * width)
+                    if b == 0:
+                        for k in range(TERMS):
+                            interleave(
+                                nc.vector.tensor_copy,
+                                term_grouped[(k, g)][:, span],
+                                term_rows[k][:, part, :, :],
+                            )
+                    attention = attention_pool.tile([P, width], BF16, tag="attention")
+                    interleave(nc.scalar.copy, attention[:], rows[:, part, :, :])
+                    if g == PASSES - 1 and part == 0:
+                        x_rows, x_codes, x_scales, diag = prepare_x(b)
 
-                products = []
-                for k in range(TERMS):
-                    product = product_pool.tile([P, GROUPED], BF16, align_bytes=64, tag="product")
-                    nc.vector.tensor_tensor(
-                        out=product[:],
-                        in0=term_grouped[(k, g)][:],
-                        in1=attention[:],
-                        op=mybir.AluOpType.mult,
-                    )
-                    products.append(product)
-                for k in range(TERMS):
-                    nc.vector.quantize_mx(
-                        out=w_codes[k][:, g, :].bitcast(FP8X4),
-                        scales=w_scales[k][:, g, :],
-                        in_=products[k][:],
-                    )
+                    products = []
+                    for k in range(TERMS):
+                        product = product_pool.tile([P, width], BF16, align_bytes=64, tag="product")
+                        nc.vector.tensor_tensor(
+                            out=product[:],
+                            in0=term_grouped[(k, g)][:, span],
+                            in1=attention[:],
+                            op=mybir.AluOpType.mult,
+                        )
+                        products.append(product)
+                    m_cols = slice(part * NODES // parts, (part + 1) * NODES // parts)
+                    for k in range(TERMS):
+                        nc.vector.quantize_mx(
+                            out=w_codes[k][:, g, m_cols].bitcast(FP8X4),
+                            scales=w_scales[k][:, g, m_cols],
+                            in_=products[k][:],
+                        )
 
             for k in range(TERMS):
                 for bank in range(BANKS):

@@ -35,6 +35,13 @@ def interleave(copy, grouped, rows):
     )
 
 
+def pair_rows(copy, paired, rows):
+    copy(
+        out=paired.rearrange("p (h w e) -> p h w e", h=2, e=2),
+        in_=rows.rearrange("p (h e) w -> p h w e", h=2),
+    )
+
+
 def tile_napl_conv_withsat_pb_t_kernel(tc, supports, cheb_2, spatial_attention, x, out):
     nc = tc.nc
     terms = (supports, cheb_2)
@@ -140,7 +147,7 @@ def tile_napl_conv_withsat_pb_t_kernel(tc, supports, cheb_2, spatial_attention, 
                                 term_rows[k][:, part, :, :],
                             )
                     attention = attention_pool.tile([P, width], BF16, tag="attention")
-                    interleave(nc.scalar.copy, attention[:], rows[:, part, :, :])
+                    pair_rows(nc.scalar.copy, attention[:], rows[:, part, :, :])
                     if g == PASSES - 1 and part == 0:
                         x_rows, x_codes, x_scales, diag = prepare_x(b)
 
@@ -148,9 +155,9 @@ def tile_napl_conv_withsat_pb_t_kernel(tc, supports, cheb_2, spatial_attention, 
                     for k in range(TERMS):
                         product = product_pool.tile([P, width], BF16, align_bytes=64, tag="product")
                         nc.vector.tensor_tensor(
-                            out=product[:],
-                            in0=term_grouped[(k, g)][:, span],
-                            in1=attention[:],
+                            out=product[:].rearrange("p (w h e) -> p w h e", h=2, e=2),
+                            in0=term_grouped[(k, g)][:, span].rearrange("p (w h e) -> p w h e", h=2, e=2),
+                            in1=attention[:].rearrange("p (h w e) -> p w h e", h=2, e=2),
                             op=mybir.AluOpType.mult,
                         )
                         products.append(product)

@@ -1,6 +1,7 @@
 from contextlib import ExitStack
 
 import concourse.mybir as mybir
+from concourse.masks import make_identity
 
 BF16 = mybir.dt.bfloat16
 F32 = mybir.dt.float32
@@ -23,7 +24,11 @@ M_TILES_PER_BANK = 4
 BANKS = NODES // (P * M_TILES_PER_BANK)
 FIRST_PARTS = 2
 LAST_PARTS = 4
+BANK_COLS = 256
+MOVE_COLS = 128
 DIAG_SLOT = 16
+
+TENSOR_PASSES = ((0, 0), (2, 1), (5, 0))
 
 FLOPS = 2 * TERMS * BATCH * NODES * NODES * CHANNELS
 
@@ -54,7 +59,9 @@ def tile_napl_conv_withsat_pb_t_kernel(tc, supports, cheb_2, spatial_attention, 
         operand_pool = ctx.enter_context(tc.tile_pool(name="operand", bufs=2))
         x_pool = ctx.enter_context(tc.tile_pool(name="x", bufs=3))
         result_pool = ctx.enter_context(tc.tile_pool(name="result", bufs=4))
-        psum = ctx.enter_context(tc.psum_pool(name="psum", bufs=6))
+        psum = ctx.enter_context(tc.psum_pool(name="psum", bufs=8))
+        identity = keep.tile([P, P], BF16)
+        make_identity(nc, identity[:])
 
         def new_rows(parts):
             rows = rows_pool.tile([P, parts, PACK, NODES // parts], BF16, tag="rows")
@@ -112,18 +119,25 @@ def tile_napl_conv_withsat_pb_t_kernel(tc, supports, cheb_2, spatial_attention, 
                 return LAST_PARTS
             return 1
 
-        for b in range(BATCH):
-            w_codes = []
-            w_scales = []
+        codes_of = {}
+        scales_of = {}
+        x_of = {}
+
+        def new_operands(b):
+            codes_of[b] = []
+            scales_of[b] = []
             for k in range(TERMS):
-                w_codes.append(
+                codes_of[b].append(
                     operand_pool.tile([P, PASSES, NODES], U32, align_bytes=64, name="w_codes%d" % k)
                 )
-                w_scales.append(
+                scales_of[b].append(
                     operand_pool.tile([P, PASSES, NODES], U8, align_bytes=64, name="w_scales%d" % k)
                 )
 
-            for g in range(PASSES):
+        def one_pass(b, g):
+                w_codes = codes_of[b]
+                w_scales = scales_of[b]
+                on_tensor = (b, g) in TENSOR_PASSES
                 parts = parts_of(b, g)
                 width = GROUPED // parts
                 rows = new_rows(parts)
@@ -146,21 +160,49 @@ def tile_napl_conv_withsat_pb_t_kernel(tc, supports, cheb_2, spatial_attention, 
                                 term_grouped[(k, g)][:, span],
                                 term_rows[k][:, part, :, :],
                             )
-                    attention = attention_pool.tile([P, width], BF16, tag="attention")
-                    pair_rows(nc.scalar.copy, attention[:], rows[:, part, :, :])
+                    if on_tensor:
+                        banks = []
+                        for c in range(0, width // PACK, BANK_COLS):
+                            bank = psum.tile([P, BANK_COLS * PACK], BF16, tag="bank")
+                            for u in range(0, BANK_COLS, MOVE_COLS):
+                                nc.tensor.matmul(
+                                    out=bank[:, u * PACK : (u + MOVE_COLS) * PACK],
+                                    lhsT=identity[:],
+                                    rhs=rows[:, part, :, c + u : c + u + MOVE_COLS].rearrange("p j w -> p w j"),
+                                    start=True,
+                                    stop=True,
+                                )
+                            banks.append(bank)
+                    else:
+                        attention = attention_pool.tile([P, width], BF16, tag="attention")
+                        pair_rows(nc.scalar.copy, attention[:], rows[:, part, :, :])
                     if g == PASSES - 1 and part == 0:
-                        x_rows, x_codes, x_scales, diag = prepare_x(b)
+                        x_of[b] = prepare_x(b)
 
                     products = []
                     for k in range(TERMS):
                         product = product_pool.tile([P, width], BF16, align_bytes=64, tag="product")
+                        products.append(product)
+                    if on_tensor:
+                        for i in range(len(banks)):
+                            for k in range(TERMS):
+                                first = i * BANK_COLS * PACK
+                                here = slice(first, first + BANK_COLS * PACK)
+                                there = slice(span.start + first, span.start + first + BANK_COLS * PACK)
+                                nc.vector.tensor_tensor(
+                                    out=products[k][:, here],
+                                    in0=term_grouped[(k, g)][:, there],
+                                    in1=banks[i][:],
+                                    op=mybir.AluOpType.mult,
+                                )
+                    for k in range(0 if on_tensor else TERMS):
+                        product = products[k]
                         nc.vector.tensor_tensor(
                             out=product[:].rearrange("p (w h e) -> p w h e", h=2, e=2),
                             in0=term_grouped[(k, g)][:, span].rearrange("p (w h e) -> p w h e", h=2, e=2),
                             in1=attention[:].rearrange("p (h w e) -> p w h e", h=2, e=2),
                             op=mybir.AluOpType.mult,
                         )
-                        products.append(product)
                     m_cols = slice(part * NODES // parts, (part + 1) * NODES // parts)
                     for k in range(TERMS):
                         nc.vector.quantize_mx(
@@ -169,9 +211,13 @@ def tile_napl_conv_withsat_pb_t_kernel(tc, supports, cheb_2, spatial_attention, 
                             in_=products[k][:],
                         )
 
+        def finish(b):
+            w_codes = codes_of[b]
+            w_scales = scales_of[b]
+            x_rows, x_codes, x_scales, diag = x_of[b]
             for k in range(TERMS):
                 for bank in range(BANKS):
-                    acc = psum.tile([P, M_TILES_PER_BANK, CHANNELS], F32)
+                    acc = psum.tile([P, M_TILES_PER_BANK, CHANNELS], F32, tag="bank")
                     for t in range(M_TILES_PER_BANK):
                         first_m = (bank * M_TILES_PER_BANK + t) * P
                         m_cols = slice(first_m, first_m + P)
@@ -205,3 +251,14 @@ def tile_napl_conv_withsat_pb_t_kernel(tc, supports, cheb_2, spatial_attention, 
                 out=out[0, b].rearrange("(g p j) f t -> p g (j f t)", g=PASSES, j=PACK),
                 in_=scaled_x[:].rearrange("p (g j) c -> p g (j c)", g=PASSES),
             )
+
+        steps = []
+        for b in range(BATCH):
+            for g in range(PASSES):
+                steps.append((b, g))
+        for b, g in steps:
+            if g == 0:
+                new_operands(b)
+            one_pass(b, g)
+            if g == PASSES - 1:
+                finish(b)

@@ -28,7 +28,7 @@ BANK_COLS = 256
 MOVE_COLS = 128
 DIAG_SLOT = 16
 
-TENSOR_PASSES = ((0, 0), (2, 1), (5, 0))
+TENSOR_PASSES = ((0, 0), (0, 1), (4, 0))
 
 FLOPS = 2 * TERMS * BATCH * NODES * NODES * CHANNELS
 
@@ -41,10 +41,7 @@ def interleave(copy, grouped, rows):
 
 
 def pair_rows(copy, paired, rows):
-    copy(
-        out=paired.rearrange("p (h w e) -> p h w e", h=2, e=2),
-        in_=rows.rearrange("p (h e) w -> p h w e", h=2),
-    )
+    copy(out=paired, in_=rows.rearrange("p (h e) w -> p h w e", h=2))
 
 
 def tile_napl_conv_withsat_pb_t_kernel(tc, supports, cheb_2, spatial_attention, x, out):
@@ -112,6 +109,12 @@ def tile_napl_conv_withsat_pb_t_kernel(tc, supports, cheb_2, spatial_attention, 
 
         term_rows = {}
 
+        def term_columns(k, g, cols):
+            if g == 0:
+                return term_grouped[(k, g)][:].rearrange("p (w h e) -> p w h e", h=2, e=2)[:, cols, :, :]
+            planes = term_grouped[(k, g)][:].rearrange("p (h w e) -> p w h e", h=2, e=2)
+            return planes[:, cols, :, :]
+
         def parts_of(b, g):
             if (b, g) == (0, 0):
                 return FIRST_PARTS
@@ -152,14 +155,18 @@ def tile_napl_conv_withsat_pb_t_kernel(tc, supports, cheb_2, spatial_attention, 
                             load_rows(term_rows[k], terms[k], g, part, parts)
                     load_rows(rows, spatial_attention[b], g, part, parts)
                 for part in range(parts):
-                    span = slice(part * width, (part + 1) * width)
+                    m_cols = slice(part * NODES // parts, (part + 1) * NODES // parts)
                     if b == 0:
                         for k in range(TERMS):
-                            interleave(
-                                nc.vector.tensor_copy,
-                                term_grouped[(k, g)][:, span],
-                                term_rows[k][:, part, :, :],
-                            )
+                            on_vector = part == 0 if g == 0 else k == 0
+                            copy = nc.vector.tensor_copy if on_vector else nc.scalar.copy
+                            grouped = term_grouped[(k, g)][:]
+                            if g == 0:
+                                span = slice(m_cols.start * PACK, m_cols.stop * PACK)
+                                interleave(copy, grouped[:, span], term_rows[k][:, part, :, :])
+                            else:
+                                planes = grouped.rearrange("p (h w e) -> p h w e", h=2, e=2)
+                                pair_rows(copy, planes, term_rows[k][:, part, :, :])
                     if on_tensor:
                         banks = []
                         for c in range(0, width // PACK, BANK_COLS):
@@ -174,7 +181,7 @@ def tile_napl_conv_withsat_pb_t_kernel(tc, supports, cheb_2, spatial_attention, 
                                 )
                             banks.append(bank)
                     else:
-                        attention = attention_pool.tile([P, width], BF16, tag="attention")
+                        attention = attention_pool.tile([P, 2, width // PACK, 2], BF16, tag="attention")
                         pair_rows(nc.scalar.copy, attention[:], rows[:, part, :, :])
                     if g == PASSES - 1 and part == 0:
                         x_of[b] = prepare_x(b)
@@ -186,24 +193,23 @@ def tile_napl_conv_withsat_pb_t_kernel(tc, supports, cheb_2, spatial_attention, 
                     if on_tensor:
                         for i in range(len(banks)):
                             for k in range(TERMS):
-                                first = i * BANK_COLS * PACK
-                                here = slice(first, first + BANK_COLS * PACK)
-                                there = slice(span.start + first, span.start + first + BANK_COLS * PACK)
+                                first = i * BANK_COLS
+                                here = slice(first * PACK, (first + BANK_COLS) * PACK)
+                                there = slice(m_cols.start + first, m_cols.start + first + BANK_COLS)
                                 nc.vector.tensor_tensor(
-                                    out=products[k][:, here],
-                                    in0=term_grouped[(k, g)][:, there],
-                                    in1=banks[i][:],
+                                    out=products[k][:, here].rearrange("p (w h e) -> p w h e", h=2, e=2),
+                                    in0=term_columns(k, g, there),
+                                    in1=banks[i][:].rearrange("p (w h e) -> p w h e", h=2, e=2),
                                     op=mybir.AluOpType.mult,
                                 )
                     for k in range(0 if on_tensor else TERMS):
                         product = products[k]
                         nc.vector.tensor_tensor(
                             out=product[:].rearrange("p (w h e) -> p w h e", h=2, e=2),
-                            in0=term_grouped[(k, g)][:, span].rearrange("p (w h e) -> p w h e", h=2, e=2),
-                            in1=attention[:].rearrange("p (h w e) -> p w h e", h=2, e=2),
+                            in0=term_columns(k, g, m_cols),
+                            in1=attention[:].rearrange("p h w e -> p w h e"),
                             op=mybir.AluOpType.mult,
                         )
-                    m_cols = slice(part * NODES // parts, (part + 1) * NODES // parts)
                     for k in range(TERMS):
                         nc.vector.quantize_mx(
                             out=w_codes[k][:, g, m_cols].bitcast(FP8X4),

@@ -110,10 +110,7 @@ def tile_napl_conv_withsat_pb_t_kernel(tc, supports, cheb_2, spatial_attention, 
         term_rows = {}
 
         def term_columns(k, g, cols):
-            if g == 0:
-                return term_grouped[(k, g)][:].rearrange("p (w h e) -> p w h e", h=2, e=2)[:, cols, :, :]
-            planes = term_grouped[(k, g)][:].rearrange("p (h w e) -> p w h e", h=2, e=2)
-            return planes[:, cols, :, :]
+            return term_grouped[(k, g)][:].rearrange("p (w h e) -> p w h e", h=2, e=2)[:, cols, :, :]
 
         def parts_of(b, g):
             if (b, g) == (0, 0):
@@ -161,12 +158,8 @@ def tile_napl_conv_withsat_pb_t_kernel(tc, supports, cheb_2, spatial_attention, 
                             on_vector = part == 0 if g == 0 else k == 0
                             copy = nc.vector.tensor_copy if on_vector else nc.scalar.copy
                             grouped = term_grouped[(k, g)][:]
-                            if g == 0:
-                                span = slice(m_cols.start * PACK, m_cols.stop * PACK)
-                                interleave(copy, grouped[:, span], term_rows[k][:, part, :, :])
-                            else:
-                                planes = grouped.rearrange("p (h w e) -> p h w e", h=2, e=2)
-                                pair_rows(copy, planes, term_rows[k][:, part, :, :])
+                            span = slice(m_cols.start * PACK, m_cols.stop * PACK)
+                            interleave(copy, grouped[:, span], term_rows[k][:, part, :, :])
                     if on_tensor:
                         banks = []
                         for c in range(0, width // PACK, BANK_COLS):

@@ -20,12 +20,9 @@ TERMS = 2
 PASSES = NODES // K_PASS
 GROUPED = NODES * PACK
 RUN = 4
-M_TILES_PER_BANK = 4
-BANKS = NODES // (P * M_TILES_PER_BANK)
-FIRST_PARTS = 2
-LAST_PARTS = 4
+OUT_COLS = 512
+LAST_WIDTHS = (512, 256, 128, 128)
 BANK_COLS = 256
-MOVE_COLS = 128
 DIAG_SLOT = 16
 
 TENSOR_PASSES = ((0, 0), (0, 1), (4, 0))
@@ -44,6 +41,13 @@ def pair_rows(copy, paired, rows):
     copy(out=paired, in_=rows.rearrange("p (h e) w -> p h w e", h=2))
 
 
+def term_shares(nc, k, g):
+    vector, scalar = nc.vector.tensor_copy, nc.scalar.copy
+    if (k, g) == (1, 0):
+        return [(vector, 0, NODES // 2), (scalar, NODES // 2, NODES)]
+    return [(scalar if (k, g) == (0, 1) else vector, 0, NODES)]
+
+
 def tile_napl_conv_withsat_pb_t_kernel(tc, supports, cheb_2, spatial_attention, x, out):
     nc = tc.nc
     terms = (supports, cheb_2)
@@ -56,20 +60,22 @@ def tile_napl_conv_withsat_pb_t_kernel(tc, supports, cheb_2, spatial_attention, 
         operand_pool = ctx.enter_context(tc.tile_pool(name="operand", bufs=2))
         x_pool = ctx.enter_context(tc.tile_pool(name="x", bufs=3))
         result_pool = ctx.enter_context(tc.tile_pool(name="result", bufs=4))
-        psum = ctx.enter_context(tc.psum_pool(name="psum", bufs=8))
+        psum = ctx.enter_context(tc.psum_pool(name="psum", bufs=4))
+        map_psum = ctx.enter_context(tc.psum_pool(name="map", bufs=4))
         identity = keep.tile([P, P], BF16)
         make_identity(nc, identity[:])
 
-        def new_rows(parts):
-            rows = rows_pool.tile([P, parts, PACK, NODES // parts], BF16, tag="rows")
+        def load_rows(matrix, g, ranges):
+            rows = rows_pool.tile([P, GROUPED], BF16, tag="rows")
+            for lo, hi in ranges:
+                nc.sync.dma_start(
+                    out=rows_in(rows, lo, hi),
+                    in_=matrix[g * K_PASS : (g + 1) * K_PASS, lo:hi].rearrange("(p j) m -> p j m", j=PACK),
+                )
             return rows
 
-        def load_rows(rows, matrix, g, part, parts):
-            cols = slice(part * NODES // parts, (part + 1) * NODES // parts)
-            nc.sync.dma_start(
-                out=rows[:, part, :, :],
-                in_=matrix[g * K_PASS : (g + 1) * K_PASS, cols].rearrange("(p j) m -> p j m", j=PACK),
-            )
+        def rows_in(rows, lo, hi):
+            return rows[:, lo * PACK : hi * PACK].rearrange("p (j w) -> p j w", j=PACK)
 
         def prepare_x(b):
             x_rows = x_pool.tile([P, PASSES * PACK, CHANNELS], BF16)
@@ -107,17 +113,28 @@ def tile_napl_conv_withsat_pb_t_kernel(tc, supports, cheb_2, spatial_attention, 
 
         term_grouped = {}
 
-        term_rows = {}
+        def term_columns(k, g, lo, hi):
+            return term_grouped[(k, g)][:, lo * PACK : hi * PACK].rearrange("p (w h e) -> p w h e", h=2, e=2)
 
-        def term_columns(k, g, cols):
-            return term_grouped[(k, g)][:].rearrange("p (w h e) -> p w h e", h=2, e=2)[:, cols, :, :]
+        def interleave_term(k, g, rows):
+            grouped = keep.tile([P, GROUPED], BF16, name="term%d_pass%d" % (k, g))
+            term_grouped[(k, g)] = grouped
+            for engine_copy, lo, hi in term_shares(nc, k, g):
+                interleave(engine_copy, grouped[:, lo * PACK : hi * PACK], rows_in(rows, 0, NODES)[:, :, lo:hi])
 
-        def parts_of(b, g):
-            if (b, g) == (0, 0):
-                return FIRST_PARTS
-            if (b, g) == (BATCH - 1, PASSES - 1):
-                return LAST_PARTS
-            return 1
+        def multiply(k, g, lo, hi, product, map_columns):
+            nc.vector.tensor_tensor(
+                out=product.rearrange("p (w h e) -> p w h e", h=2, e=2),
+                in0=term_columns(k, g, lo, hi),
+                in1=map_columns,
+                op=mybir.AluOpType.mult,
+            )
+
+        def ranges_of(b, g):
+            if (b, g) != (BATCH - 1, PASSES - 1):
+                return [(0, NODES)]
+            starts = [sum(LAST_WIDTHS[:i]) for i in range(len(LAST_WIDTHS))]
+            return [(start, start + width) for start, width in zip(starts, LAST_WIDTHS)]
 
         codes_of = {}
         scales_of = {}
@@ -134,92 +151,87 @@ def tile_napl_conv_withsat_pb_t_kernel(tc, supports, cheb_2, spatial_attention, 
                     operand_pool.tile([P, PASSES, NODES], U8, align_bytes=64, name="w_scales%d" % k)
                 )
 
-        def one_pass(b, g):
-                w_codes = codes_of[b]
-                w_scales = scales_of[b]
-                on_tensor = (b, g) in TENSOR_PASSES
-                parts = parts_of(b, g)
-                width = GROUPED // parts
-                rows = new_rows(parts)
-                if b == 0:
-                    for k in range(TERMS):
-                        term_rows[k] = new_rows(parts)
-                        grouped = keep.tile([P, GROUPED], BF16, name="term%d_pass%d" % (k, g))
-                        term_grouped[(k, g)] = grouped
-                for part in range(parts):
-                    if b == 0:
-                        for k in range(TERMS):
-                            load_rows(term_rows[k], terms[k], g, part, parts)
-                    load_rows(rows, spatial_attention[b], g, part, parts)
-                for part in range(parts):
-                    m_cols = slice(part * NODES // parts, (part + 1) * NODES // parts)
-                    if b == 0:
-                        for k in range(TERMS):
-                            on_vector = part == 0 if g == 0 else k == 0
-                            copy = nc.vector.tensor_copy if on_vector else nc.scalar.copy
-                            grouped = term_grouped[(k, g)][:]
-                            span = slice(m_cols.start * PACK, m_cols.stop * PACK)
-                            interleave(copy, grouped[:, span], term_rows[k][:, part, :, :])
-                    if on_tensor:
-                        banks = []
-                        for c in range(0, width // PACK, BANK_COLS):
-                            bank = psum.tile([P, BANK_COLS * PACK], BF16, tag="bank")
-                            for u in range(0, BANK_COLS, MOVE_COLS):
-                                nc.tensor.matmul(
-                                    out=bank[:, u * PACK : (u + MOVE_COLS) * PACK],
-                                    lhsT=identity[:],
-                                    rhs=rows[:, part, :, c + u : c + u + MOVE_COLS].rearrange("p j w -> p w j"),
-                                    start=True,
-                                    stop=True,
-                                )
-                            banks.append(bank)
-                    else:
-                        attention = attention_pool.tile([P, 2, width // PACK, 2], BF16, tag="attention")
-                        pair_rows(nc.scalar.copy, attention[:], rows[:, part, :, :])
-                    if g == PASSES - 1 and part == 0:
-                        x_of[b] = prepare_x(b)
+        def out_ranges(b):
+            ranges = []
+            for lo, hi in ranges_of(b, PASSES - 1):
+                ranges += [(first, min(first + OUT_COLS, hi)) for first in range(lo, hi, OUT_COLS)]
+            return ranges
 
-                    products = []
-                    for k in range(TERMS):
-                        product = product_pool.tile([P, width], BF16, align_bytes=64, tag="product")
-                        products.append(product)
-                    if on_tensor:
-                        for i in range(len(banks)):
-                            for k in range(TERMS):
-                                first = i * BANK_COLS
-                                here = slice(first * PACK, (first + BANK_COLS) * PACK)
-                                there = slice(m_cols.start + first, m_cols.start + first + BANK_COLS)
-                                nc.vector.tensor_tensor(
-                                    out=products[k][:, here].rearrange("p (w h e) -> p w h e", h=2, e=2),
-                                    in0=term_columns(k, g, there),
-                                    in1=banks[i][:].rearrange("p (w h e) -> p w h e", h=2, e=2),
-                                    op=mybir.AluOpType.mult,
-                                )
-                    for k in range(0 if on_tensor else TERMS):
-                        product = products[k]
-                        nc.vector.tensor_tensor(
-                            out=product[:].rearrange("p (w h e) -> p w h e", h=2, e=2),
-                            in0=term_columns(k, g, m_cols),
-                            in1=attention[:].rearrange("p h w e -> p w h e"),
-                            op=mybir.AluOpType.mult,
-                        )
-                    for k in range(TERMS):
-                        nc.vector.quantize_mx(
-                            out=w_codes[k][:, g, m_cols].bitcast(FP8X4),
-                            scales=w_scales[k][:, g, m_cols],
-                            in_=products[k][:],
-                        )
+        def quantise(b, k, g, lo, hi, product):
+            nc.vector.quantize_mx(
+                out=codes_of[b][k][:, g, lo:hi].bitcast(FP8X4),
+                scales=scales_of[b][k][:, g, lo:hi],
+                in_=product,
+            )
+
+        def move_map(rows):
+            banks = []
+            for lo in range(0, NODES, BANK_COLS):
+                bank = map_psum.tile([P, BANK_COLS, 2, 2], BF16)
+                for h in range(2):
+                    nc.tensor.matmul(
+                        out=bank[:, :, h, :],
+                        lhsT=identity[:],
+                        rhs=rows_in(rows, 0, NODES)[:, 2 * h : 2 * h + 2, lo : lo + BANK_COLS].rearrange(
+                            "p e w -> p w e"
+                        ),
+                        start=True,
+                        stop=True,
+                    )
+                banks.append(bank)
+            return banks
+
+        def one_pass(b, g):
+            ranges = ranges_of(b, g)
+            term_rows = {}
+            if b == 0:
+                term_rows[0] = load_rows(terms[0], g, ranges)
+                if g == 1:
+                    term_rows[1] = load_rows(terms[1], g, ranges)
+            rows = load_rows(spatial_attention[b], g, ranges)
+            if b == 0 and g == 0:
+                term_rows[1] = load_rows(terms[1], g, ranges)
+
+            if (b, g) in TENSOR_PASSES:
+                banks = move_map(rows)
+                if g == PASSES - 1:
+                    x_of[b] = prepare_x(b)
+                products = []
+                for k in range(TERMS):
+                    product = product_pool.tile([P, GROUPED], BF16, align_bytes=64, tag="product")
+                    products.append(product)
+                    if b == 0:
+                        interleave_term(k, g, term_rows[k])
+                    for i in range(len(banks)):
+                        lo, hi = i * BANK_COLS, (i + 1) * BANK_COLS
+                        multiply(k, g, lo, hi, product[:, lo * PACK : hi * PACK], banks[i][:])
+                for k in range(TERMS):
+                    quantise(b, k, g, 0, NODES, products[k][:])
+                return
+
+            for lo, hi in ranges:
+                attention = attention_pool.tile([P, 2, hi - lo, 2], BF16, tag="attention")
+                pair_rows(nc.scalar.copy, attention[:], rows_in(rows, lo, hi))
+                if g == PASSES - 1 and lo == 0:
+                    x_of[b] = prepare_x(b)
+                products = []
+                for k in range(TERMS):
+                    product = product_pool.tile([P, (hi - lo) * PACK], BF16, align_bytes=64, tag="product")
+                    products.append(product)
+                    multiply(k, g, lo, hi, product[:], attention[:].rearrange("p h w e -> p w h e"))
+                for k in range(TERMS):
+                    quantise(b, k, g, lo, hi, products[k][:])
 
         def finish(b):
             w_codes = codes_of[b]
             w_scales = scales_of[b]
             x_rows, x_codes, x_scales, diag = x_of[b]
-            for k in range(TERMS):
-                for bank in range(BANKS):
-                    acc = psum.tile([P, M_TILES_PER_BANK, CHANNELS], F32, tag="bank")
-                    for t in range(M_TILES_PER_BANK):
-                        first_m = (bank * M_TILES_PER_BANK + t) * P
-                        m_cols = slice(first_m, first_m + P)
+            for lo, hi in out_ranges(b):
+                for k in range(TERMS):
+                    tiles = (hi - lo) // P
+                    acc = psum.tile([P, tiles, CHANNELS], F32, tag="acc")
+                    for t in range(tiles):
+                        m_cols = slice(lo + t * P, lo + (t + 1) * P)
                         for g in range(PASSES):
                             nc.tensor.matmul_mx(
                                 out=acc[:, t, :],
@@ -230,11 +242,10 @@ def tile_napl_conv_withsat_pb_t_kernel(tc, supports, cheb_2, spatial_attention, 
                                 start=(g == 0),
                                 stop=(g == PASSES - 1),
                             )
-                    result = result_pool.tile([P, M_TILES_PER_BANK, CHANNELS], F32)
+                    result = result_pool.tile([P, tiles, CHANNELS], F32, tag="result")
                     nc.scalar.copy(out=result[:], in_=acc[:])
-                    bank_nodes = slice(bank * M_TILES_PER_BANK * P, (bank + 1) * M_TILES_PER_BANK * P)
                     nc.sync.dma_start(
-                        out=out[1 + k, b, bank_nodes].rearrange("(t q) f s -> q t (f s)", q=P),
+                        out=out[1 + k, b, lo:hi].rearrange("(t q) f s -> q t (f s)", q=P),
                         in_=result[:],
                     )
 
@@ -251,13 +262,8 @@ def tile_napl_conv_withsat_pb_t_kernel(tc, supports, cheb_2, spatial_attention, 
                 in_=scaled_x[:].rearrange("p (g j) c -> p g (j c)", g=PASSES),
             )
 
-        steps = []
         for b in range(BATCH):
+            new_operands(b)
             for g in range(PASSES):
-                steps.append((b, g))
-        for b, g in steps:
-            if g == 0:
-                new_operands(b)
-            one_pass(b, g)
-            if g == PASSES - 1:
-                finish(b)
+                one_pass(b, g)
+            finish(b)

@@ -21,11 +21,11 @@ PASSES = NODES // K_PASS
 GROUPED = NODES * PACK
 RUN = 4
 OUT_COLS = 512
-LAST_WIDTHS = (512, 256, 128, 128)
 BANK_COLS = 256
-DIAG_SLOT = 16
-
-TENSOR_PASSES = ((0, 0), (0, 1), (4, 0))
+DIAG_WINDOW = 16
+DIAG_STRIDE = PACK * DIAG_WINDOW + DIAG_WINDOW - PACK
+LAST_WIDTHS = (512, 256, 128, 128)
+TENSOR_PASSES = ((1, 0), (3, 0), (5, 0))
 
 FLOPS = 2 * TERMS * BATCH * NODES * NODES * CHANNELS
 
@@ -41,16 +41,14 @@ def pair_rows(copy, paired, rows):
     copy(out=paired, in_=rows.rearrange("p (h e) w -> p h w e", h=2))
 
 
-def term_shares(nc, k, g):
-    vector, scalar = nc.vector.tensor_copy, nc.scalar.copy
-    if (k, g) == (1, 0):
-        return [(vector, 0, NODES // 2), (scalar, NODES // 2, NODES)]
-    return [(scalar if (k, g) == (0, 1) else vector, 0, NODES)]
-
-
 def tile_napl_conv_withsat_pb_t_kernel(tc, supports, cheb_2, spatial_attention, x, out):
     nc = tc.nc
     terms = (supports, cheb_2)
+
+    steps = [(0, 0), (1, 0), (0, 1), (1, 1)] + [(b, g) for b in range(2, BATCH) for g in range(PASSES)]
+    finish = {b: steps.index((b, PASSES - 1)) for b in range(BATCH)}
+    sample_finishing = {step: b for b, step in finish.items()}
+    last_step = len(steps) - 1
 
     with ExitStack() as ctx:
         keep = ctx.enter_context(tc.tile_pool(name="keep", bufs=1))
@@ -58,202 +56,186 @@ def tile_napl_conv_withsat_pb_t_kernel(tc, supports, cheb_2, spatial_attention, 
         attention_pool = ctx.enter_context(tc.tile_pool(name="attention", bufs=3))
         product_pool = ctx.enter_context(tc.tile_pool(name="product", bufs=4))
         operand_pool = ctx.enter_context(tc.tile_pool(name="operand", bufs=2))
-        x_pool = ctx.enter_context(tc.tile_pool(name="x", bufs=3))
+        x_pool = ctx.enter_context(tc.tile_pool(name="x", bufs=4))
         result_pool = ctx.enter_context(tc.tile_pool(name="result", bufs=4))
         psum = ctx.enter_context(tc.psum_pool(name="psum", bufs=4))
         map_psum = ctx.enter_context(tc.psum_pool(name="map", bufs=4))
         identity = keep.tile([P, P], BF16)
         make_identity(nc, identity[:])
+        ctx.enter_context(tc.manual_schedule())
 
-        def load_rows(matrix, g, ranges):
-            rows = rows_pool.tile([P, GROUPED], BF16, tag="rows")
-            for lo, hi in ranges:
-                nc.sync.dma_start(
-                    out=rows_in(rows, lo, hi),
-                    in_=matrix[g * K_PASS : (g + 1) * K_PASS, lo:hi].rearrange("(p j) m -> p j m", j=PACK),
-                )
+        def column_ranges(i):
+            if i != last_step:
+                return [(0, NODES)]
+            starts = [sum(LAST_WIDTHS[:n]) for n in range(len(LAST_WIDTHS))]
+            return [(start, start + width) for start, width in zip(starts, LAST_WIDTHS)]
+
+        def load_rows(matrix, g):
+            rows = rows_pool.tile([P, PACK, NODES], BF16, tag="rows")
+            nc.sync.dma_start(
+                out=rows[:], in_=matrix[g * K_PASS : (g + 1) * K_PASS, :].rearrange("(p j) m -> p j m", j=PACK)
+            )
             return rows
 
-        def rows_in(rows, lo, hi):
-            return rows[:, lo * PACK : hi * PACK].rearrange("p (j w) -> p j w", j=PACK)
+        map_rows = {}
 
-        def prepare_x(b):
-            x_rows = x_pool.tile([P, PASSES * PACK, CHANNELS], BF16)
+        def load_map(i):
+            b, g = steps[i]
+            map_rows[i] = load_rows(spatial_attention[b], g)
+
+        x_rows = {}
+
+        def load_x(b):
+            x_rows[b] = x_pool.tile([P, PASSES * PACK, CHANNELS], BF16, name="x_rows")
             nc.sync.dma_start(
-                out=x_rows[:].rearrange("p (g j) c -> p g (j c)", g=PASSES),
+                out=x_rows[b][:].rearrange("p (g j) c -> p g (j c)", g=PASSES),
                 in_=x[b].rearrange("(g p j) f t -> p g (j f t)", g=PASSES, j=PACK),
             )
-            x_grouped = x_pool.tile([P, PASSES, CHANNELS * PACK], BF16, align_bytes=64)
+
+        diag_windows = {}
+
+        def load_diagonal(b):
+            window = x_pool.tile([P, PASSES * DIAG_STRIDE], BF16, name="diag_window")
+            diag_windows[b] = window
+            flat_map = spatial_attention[b].rearrange("n m -> (n m)")
+            block = PACK * (NODES + 1)
             for g in range(PASSES):
-                interleave(nc.scalar.copy, x_grouped[:, g, :], x_rows[:, g * PACK : (g + 1) * PACK, :])
+                if g == 0:
+                    half, row_start, first = flat_map[: P * block], 0, 0
+                else:
+                    half, row_start, first = flat_map[NODES * NODES - P * block :], PACK, NODES - DIAG_WINDOW
+                size = PACK * DIAG_WINDOW
+                nc.sync.dma_start(
+                    out=window[:, g * size : (g + 1) * size].rearrange("p (j c) -> p j c", j=PACK),
+                    in_=half.rearrange("(p s) -> p s", p=P)[:, row_start : row_start + PACK * NODES].rearrange(
+                        "p (j m) -> p j m", j=PACK
+                    )[:, :, first : first + DIAG_WINDOW],
+                )
+
+        term_rows = {}
+        term_grouped = {}
+
+        def load_term(k, g):
+            term_rows[(k, g)] = load_rows(terms[k], g)
+
+        def interleave_term(copy, k, g):
+            grouped = keep.tile([P, GROUPED], BF16, name="term%d_pass%d" % (k, g))
+            interleave(copy, grouped[:], term_rows[(k, g)][:])
+            term_grouped[(k, g)] = grouped
+
+        fed = {}
+
+        def feed(i):
+            b, g = steps[i]
+            fed[i] = []
+            if (b, g) in TENSOR_PASSES:
+                rows = map_rows[i][:]
+                for lo in range(0, NODES, BANK_COLS):
+                    bank = map_psum.tile([P, BANK_COLS, 2, 2], BF16)
+                    for h in range(2):
+                        nc.tensor.matmul(
+                            out=bank[:, :, h, :],
+                            lhsT=identity[:],
+                            rhs=rows[:, 2 * h : 2 * h + 2, lo : lo + BANK_COLS].rearrange("p e w -> p w e"),
+                            start=True,
+                            stop=True,
+                        )
+                    fed[i].append((lo, lo + BANK_COLS, bank[:]))
+            else:
+                attention = attention_pool.tile([P, 2, NODES, 2], BF16)
+                pair_rows(nc.scalar.copy, attention[:], map_rows[i][:])
+                fed[i].append((0, NODES, attention[:].rearrange("p h w e -> p w h e")))
+
+        x_grouped = {}
+
+        def interleave_x(b):
+            x_grouped[b] = x_pool.tile([P, PASSES, CHANNELS * PACK], BF16, align_bytes=64, name="x_grouped")
+            for g in range(PASSES):
+                interleave(nc.scalar.copy, x_grouped[b][:, g, :], x_rows[b][:, g * PACK : (g + 1) * PACK, :])
+
+        x_operand = {}
+
+        def quantise_x(b):
             x_codes = x_pool.tile([P, PASSES, CHANNELS], U32, align_bytes=64)
             x_scales = x_pool.tile([P, PASSES, CHANNELS], U8, align_bytes=64)
             nc.vector.quantize_mx(
                 out=x_codes[:].rearrange("p g c -> p (g c)").bitcast(FP8X4),
                 scales=x_scales[:].rearrange("p g c -> p (g c)"),
-                in_=x_grouped[:].rearrange("p g v -> p (g v)"),
+                in_=x_grouped[b][:].rearrange("p g v -> p (g v)"),
             )
-            diag_bf16 = x_pool.tile([P, PASSES, PACK, DIAG_SLOT], BF16)
-            flat_map = spatial_attention[b].rearrange("n m -> (n m)")
-            with nc.allow_non_contiguous_dma(reason="the diagonal has one value in each row"):
-                for g in range(PASSES):
-                    first = g * K_PASS * (NODES + 1)
-                    last = first + (K_PASS - 1) * (NODES + 1)
-                    nc.sync.dma_start(
-                        out=diag_bf16[:, g, :, 0:1],
-                        in_=flat_map[first : last + 1 : NODES + 1].rearrange(
-                            "(p j o) -> p j o", j=PACK, o=1
-                        ),
-                    )
-            diag = x_pool.tile([P, PASSES * PACK], F32)
-            nc.scalar.copy(
-                out=diag[:].rearrange("p (g j) -> p g j", g=PASSES), in_=diag_bf16[:, :, :, 0]
-            )
-            return x_rows, x_codes, x_scales, diag
+            x_operand[b] = (x_codes, x_scales)
 
-        term_grouped = {}
-
-        def term_columns(k, g, lo, hi):
-            return term_grouped[(k, g)][:, lo * PACK : hi * PACK].rearrange("p (w h e) -> p w h e", h=2, e=2)
-
-        def interleave_term(k, g, rows):
-            grouped = keep.tile([P, GROUPED], BF16, name="term%d_pass%d" % (k, g))
-            term_grouped[(k, g)] = grouped
-            for engine_copy, lo, hi in term_shares(nc, k, g):
-                interleave(engine_copy, grouped[:, lo * PACK : hi * PACK], rows_in(rows, 0, NODES)[:, :, lo:hi])
-
-        def multiply(k, g, lo, hi, product, map_columns):
-            nc.vector.tensor_tensor(
-                out=product.rearrange("p (w h e) -> p w h e", h=2, e=2),
-                in0=term_columns(k, g, lo, hi),
-                in1=map_columns,
-                op=mybir.AluOpType.mult,
-            )
-
-        def ranges_of(b, g):
-            if (b, g) != (BATCH - 1, PASSES - 1):
-                return [(0, NODES)]
-            starts = [sum(LAST_WIDTHS[:i]) for i in range(len(LAST_WIDTHS))]
-            return [(start, start + width) for start, width in zip(starts, LAST_WIDTHS)]
-
-        codes_of = {}
-        scales_of = {}
-        x_of = {}
+        operands = {}
 
         def new_operands(b):
-            codes_of[b] = []
-            scales_of[b] = []
+            operands[b] = []
             for k in range(TERMS):
-                codes_of[b].append(
-                    operand_pool.tile([P, PASSES, NODES], U32, align_bytes=64, name="w_codes%d" % k)
-                )
-                scales_of[b].append(
-                    operand_pool.tile([P, PASSES, NODES], U8, align_bytes=64, name="w_scales%d" % k)
-                )
+                codes = operand_pool.tile([P, PASSES, NODES], U32, align_bytes=64, name="w_codes%d" % k)
+                scales = operand_pool.tile([P, PASSES, NODES], U8, align_bytes=64, name="w_scales%d" % k)
+                operands[b].append((codes, scales))
 
-        def out_ranges(b):
-            ranges = []
-            for lo, hi in ranges_of(b, PASSES - 1):
-                ranges += [(first, min(first + OUT_COLS, hi)) for first in range(lo, hi, OUT_COLS)]
-            return ranges
+        def new_product(lo, hi):
+            product = product_pool.tile([P, (hi - lo) * PACK], BF16, align_bytes=64, tag="product")
+            return product
 
-        def quantise(b, k, g, lo, hi, product):
+        def multiply(i, k, product, lo, hi, start=0):
+            for fed_lo, fed_hi, map_columns in fed[i]:
+                first, end = max(lo, fed_lo), min(hi, fed_hi)
+                if first < end:
+                    span = slice(first * PACK, end * PACK)
+                    here = slice((first - start) * PACK, (end - start) * PACK)
+                    nc.vector.tensor_tensor(
+                        out=product[:, here].rearrange("p (w h e) -> p w h e", h=2, e=2),
+                        in0=term_grouped[(k, steps[i][1])][:, span].rearrange("p (w h e) -> p w h e", h=2, e=2),
+                        in1=map_columns[:, first - fed_lo : end - fed_lo, :, :],
+                        op=mybir.AluOpType.mult,
+                    )
+
+        def quantise(i, k, product, lo, hi):
+            b, g = steps[i]
+            codes, scales = operands[b][k]
             nc.vector.quantize_mx(
-                out=codes_of[b][k][:, g, lo:hi].bitcast(FP8X4),
-                scales=scales_of[b][k][:, g, lo:hi],
-                in_=product,
+                out=codes[:, g, lo:hi].bitcast(FP8X4), scales=scales[:, g, lo:hi], in_=product[:]
             )
 
-        def move_map(rows):
-            banks = []
-            for lo in range(0, NODES, BANK_COLS):
-                bank = map_psum.tile([P, BANK_COLS, 2, 2], BF16)
-                for h in range(2):
-                    nc.tensor.matmul(
-                        out=bank[:, :, h, :],
-                        lhsT=identity[:],
-                        rhs=rows_in(rows, 0, NODES)[:, 2 * h : 2 * h + 2, lo : lo + BANK_COLS].rearrange(
-                            "p e w -> p w e"
-                        ),
-                        start=True,
-                        stop=True,
+        def contract(b, k, lo, hi):
+            codes, scales = operands[b][k]
+            x_codes, x_scales = x_operand[b]
+            acc = psum.tile([P, (hi - lo) // P, CHANNELS], F32, tag="acc")
+            for t in range((hi - lo) // P):
+                m_cols = slice(lo + t * P, lo + (t + 1) * P)
+                for g in range(PASSES):
+                    nc.tensor.matmul_mx(
+                        out=acc[:, t, :],
+                        lhsT=codes[:, g, m_cols].bitcast(FP8X4),
+                        lhsT_scale=scales[:, g, m_cols],
+                        rhs=x_codes[:, g, :].bitcast(FP8X4),
+                        rhs_scale=x_scales[:, g, :],
+                        start=(g == 0),
+                        stop=(g == PASSES - 1),
                     )
-                banks.append(bank)
-            return banks
+            return b, k, lo, hi, acc
 
-        def one_pass(b, g):
-            ranges = ranges_of(b, g)
-            term_rows = {}
-            if b == 0:
-                term_rows[0] = load_rows(terms[0], g, ranges)
-                if g == 1:
-                    term_rows[1] = load_rows(terms[1], g, ranges)
-            rows = load_rows(spatial_attention[b], g, ranges)
-            if b == 0 and g == 0:
-                term_rows[1] = load_rows(terms[1], g, ranges)
+        def store(b, k, lo, hi, acc):
+            result = result_pool.tile([P, (hi - lo) // P, CHANNELS], F32, tag="result")
+            nc.scalar.copy(out=result[:], in_=acc[:])
+            nc.sync.dma_start(
+                out=out[1 + k, b, lo:hi].rearrange("(t q) f s -> q t (f s)", q=P), in_=result[:]
+            )
 
-            if (b, g) in TENSOR_PASSES:
-                banks = move_map(rows)
-                if g == PASSES - 1:
-                    x_of[b] = prepare_x(b)
-                products = []
-                for k in range(TERMS):
-                    product = product_pool.tile([P, GROUPED], BF16, align_bytes=64, tag="product")
-                    products.append(product)
-                    if b == 0:
-                        interleave_term(k, g, term_rows[k])
-                    for i in range(len(banks)):
-                        lo, hi = i * BANK_COLS, (i + 1) * BANK_COLS
-                        multiply(k, g, lo, hi, product[:, lo * PACK : hi * PACK], banks[i][:])
-                for k in range(TERMS):
-                    quantise(b, k, g, 0, NODES, products[k][:])
-                return
-
-            for lo, hi in ranges:
-                attention = attention_pool.tile([P, 2, hi - lo, 2], BF16, tag="attention")
-                pair_rows(nc.scalar.copy, attention[:], rows_in(rows, lo, hi))
-                if g == PASSES - 1 and lo == 0:
-                    x_of[b] = prepare_x(b)
-                products = []
-                for k in range(TERMS):
-                    product = product_pool.tile([P, (hi - lo) * PACK], BF16, align_bytes=64, tag="product")
-                    products.append(product)
-                    multiply(k, g, lo, hi, product[:], attention[:].rearrange("p h w e -> p w h e"))
-                for k in range(TERMS):
-                    quantise(b, k, g, lo, hi, products[k][:])
-
-        def finish(b):
-            w_codes = codes_of[b]
-            w_scales = scales_of[b]
-            x_rows, x_codes, x_scales, diag = x_of[b]
-            for lo, hi in out_ranges(b):
-                for k in range(TERMS):
-                    tiles = (hi - lo) // P
-                    acc = psum.tile([P, tiles, CHANNELS], F32, tag="acc")
-                    for t in range(tiles):
-                        m_cols = slice(lo + t * P, lo + (t + 1) * P)
-                        for g in range(PASSES):
-                            nc.tensor.matmul_mx(
-                                out=acc[:, t, :],
-                                lhsT=w_codes[k][:, g, m_cols].bitcast(FP8X4),
-                                lhsT_scale=w_scales[k][:, g, m_cols],
-                                rhs=x_codes[:, g, :].bitcast(FP8X4),
-                                rhs_scale=x_scales[:, g, :],
-                                start=(g == 0),
-                                stop=(g == PASSES - 1),
-                            )
-                    result = result_pool.tile([P, tiles, CHANNELS], F32, tag="result")
-                    nc.scalar.copy(out=result[:], in_=acc[:])
-                    nc.sync.dma_start(
-                        out=out[1 + k, b, lo:hi].rearrange("(t q) f s -> q t (f s)", q=P),
-                        in_=result[:],
-                    )
-
+        def scale_x(b):
+            diag = x_pool.tile([P, PASSES * PACK], F32)
+            nc.scalar.copy(
+                out=diag[:].rearrange("p (g j) -> p g j", g=PASSES),
+                in_=diag_windows[b][:].rearrange("p (g s) -> p g s", g=PASSES)[
+                    :, :, 0 : (PACK - 1) * (DIAG_WINDOW + 1) + 1 : DIAG_WINDOW + 1
+                ],
+            )
             scaled_x = result_pool.tile([P, PASSES * PACK, CHANNELS], F32)
             for s in range(PASSES * PACK):
                 nc.scalar.activation(
                     out=scaled_x[:, s, :],
-                    in_=x_rows[:, s, :],
+                    in_=x_rows[b][:, s, :],
                     func=mybir.ActivationFunctionType.Copy,
                     scale=diag[:, s : s + 1],
                 )
@@ -262,8 +244,78 @@ def tile_napl_conv_withsat_pb_t_kernel(tc, supports, cheb_2, spatial_attention, 
                 in_=scaled_x[:].rearrange("p (g j) c -> p g (j c)", g=PASSES),
             )
 
-        for b in range(BATCH):
-            new_operands(b)
-            for g in range(PASSES):
-                one_pass(b, g)
-            finish(b)
+        load_map(0)
+        load_term(0, 0)
+        load_term(1, 0)
+        load_term(0, 1)
+        load_map(1)
+        load_term(1, 1)
+        feed(0)
+        interleave_term(nc.vector.tensor_copy, 0, 0)
+        interleave_term(nc.scalar.copy, 1, 0)
+        feed(1)
+        new_operands(0)
+        products = [new_product(0, NODES) for k in range(TERMS)]
+        multiply(0, 0, products[0], 0, NODES)
+        interleave_term(nc.vector.tensor_copy, 0, 1)
+        multiply(0, 1, products[1], 0, NODES)
+        interleave_term(nc.scalar.copy, 1, 1)
+        load_map(2)
+        load_x(0)
+        feed(2)
+        for i in range(3, 6):
+            load_map(i)
+        load_x(1)
+        for k in range(TERMS):
+            quantise(0, k, products[k], 0, NODES)
+
+        waiting = []
+        for i in range(1, last_step + 1):
+            b, g = steps[i]
+            if b not in operands:
+                new_operands(b)
+            if i + 5 <= last_step:
+                load_map(i + 5)
+            if sample_finishing.get(i + 4, 0) >= 2:
+                load_x(sample_finishing[i + 4])
+            if i == 1:
+                load_diagonal(0)
+            if i + 2 in sample_finishing and sample_finishing[i + 2] > 0:
+                load_diagonal(sample_finishing[i + 2])
+
+            if i == 1:
+                interleave_x(0)
+            if i + 2 <= last_step:
+                feed(i + 2)
+            for group in waiting:
+                store(*group)
+            waiting = []
+            if i == 2:
+                interleave_x(1)
+            if i in (3, 4):
+                scale_x(i - 3)
+            if i == 3 or (i > 4 and i in sample_finishing and i < last_step):
+                interleave_x(b + 1)
+            if i > 4 and i in sample_finishing and i < last_step:
+                scale_x(b)
+            if i == last_step - 1:
+                scale_x(BATCH - 1)
+
+            for first, end in column_ranges(i):
+                products = [new_product(first, end) for k in range(TERMS)]
+                pieces = [(max(first, lo), min(end, hi)) for lo, hi, columns in fed[i]]
+                for lo, hi in pieces:
+                    for k in range(TERMS):
+                        multiply(i, k, products[k], lo, hi, first)
+                if first == 0 and i in sample_finishing:
+                    quantise_x(b)
+                for k in range(TERMS):
+                    quantise(i, k, products[k], first, end)
+                if i in sample_finishing:
+                    for k in range(TERMS):
+                        for lo in range(first, end, OUT_COLS):
+                            group = contract(b, k, lo, min(lo + OUT_COLS, end))
+                            if i == last_step:
+                                store(*group)
+                            else:
+                                waiting.append(group)

@@ -25,7 +25,10 @@ BANK_COLS = 256
 DIAG_WINDOW = 16
 DIAG_STRIDE = PACK * DIAG_WINDOW + DIAG_WINDOW - PACK
 LAST_WIDTHS = (512, 256, 128, 128)
-TENSOR_PASSES = ((1, 0), (3, 0), (5, 0))
+TENSOR_PASSES = ((1, 0), (0, 1), (4, 0))
+
+HALVES = ((0, NODES // 2), (NODES // 2, NODES))
+LEADING = 3
 
 FLOPS = 2 * TERMS * BATCH * NODES * NODES * CHANNELS
 
@@ -45,19 +48,22 @@ def tile_napl_conv_withsat_pb_t_kernel(tc, supports, cheb_2, spatial_attention, 
     nc = tc.nc
     terms = (supports, cheb_2)
 
-    steps = [(0, 0), (1, 0), (0, 1), (1, 1)] + [(b, g) for b in range(2, BATCH) for g in range(PASSES)]
+    leading = range(LEADING)
+    steps = [(b, g) for g in range(PASSES) for b in leading]
+    steps += [(b, g) for b in range(LEADING, BATCH) for g in range(PASSES)]
     finish = {b: steps.index((b, PASSES - 1)) for b in range(BATCH)}
     sample_finishing = {step: b for b, step in finish.items()}
     last_step = len(steps) - 1
 
     with ExitStack() as ctx:
         keep = ctx.enter_context(tc.tile_pool(name="keep", bufs=1))
-        rows_pool = ctx.enter_context(tc.tile_pool(name="rows", bufs=6))
+        rows_pool = ctx.enter_context(tc.tile_pool(name="rows", bufs=5))
         attention_pool = ctx.enter_context(tc.tile_pool(name="attention", bufs=3))
         product_pool = ctx.enter_context(tc.tile_pool(name="product", bufs=4))
-        operand_pool = ctx.enter_context(tc.tile_pool(name="operand", bufs=2))
+        operand_pool = ctx.enter_context(tc.tile_pool(name="operand", bufs=3))
         x_pool = ctx.enter_context(tc.tile_pool(name="x", bufs=4))
         result_pool = ctx.enter_context(tc.tile_pool(name="result", bufs=4))
+        scaled_pool = ctx.enter_context(tc.tile_pool(name="scaled", bufs=2))
         psum = ctx.enter_context(tc.psum_pool(name="psum", bufs=4))
         map_psum = ctx.enter_context(tc.psum_pool(name="map", bufs=4))
         identity = keep.tile([P, P], BF16)
@@ -70,18 +76,25 @@ def tile_napl_conv_withsat_pb_t_kernel(tc, supports, cheb_2, spatial_attention, 
             starts = [sum(LAST_WIDTHS[:n]) for n in range(len(LAST_WIDTHS))]
             return [(start, start + width) for start, width in zip(starts, LAST_WIDTHS)]
 
-        def load_rows(matrix, g):
-            rows = rows_pool.tile([P, PACK, NODES], BF16, tag="rows")
-            nc.sync.dma_start(
-                out=rows[:], in_=matrix[g * K_PASS : (g + 1) * K_PASS, :].rearrange("(p j) m -> p j m", j=PACK)
-            )
+        def new_rows():
+            rows = rows_pool.tile([P, GROUPED], BF16, tag="rows")
             return rows
+
+        def rows_in(rows, lo, hi):
+            return rows[:, lo * PACK : hi * PACK].rearrange("p (j w) -> p j w", j=PACK)
+
+        def load_columns(rows, matrix, g, lo, hi):
+            nc.sync.dma_start(
+                out=rows_in(rows, lo, hi),
+                in_=matrix[g * K_PASS : (g + 1) * K_PASS, lo:hi].rearrange("(p j) m -> p j m", j=PACK),
+            )
 
         map_rows = {}
 
         def load_map(i):
             b, g = steps[i]
-            map_rows[i] = load_rows(spatial_attention[b], g)
+            map_rows[i] = new_rows()
+            load_columns(map_rows[i], spatial_attention[b], g, 0, NODES)
 
         x_rows = {}
 
@@ -116,12 +129,13 @@ def tile_napl_conv_withsat_pb_t_kernel(tc, supports, cheb_2, spatial_attention, 
         term_grouped = {}
 
         def load_term(k, g):
-            term_rows[(k, g)] = load_rows(terms[k], g)
+            term_rows[(k, g)] = new_rows()
+            load_columns(term_rows[(k, g)], terms[k], g, 0, NODES)
 
-        def interleave_term(copy, k, g):
-            grouped = keep.tile([P, GROUPED], BF16, name="term%d_pass%d" % (k, g))
-            interleave(copy, grouped[:], term_rows[(k, g)][:])
-            term_grouped[(k, g)] = grouped
+        def interleave_term(copy, k, g, lo, hi, rows):
+            if (k, g) not in term_grouped:
+                term_grouped[(k, g)] = keep.tile([P, GROUPED], BF16, name="term%d_pass%d" % (k, g))
+            interleave(copy, term_grouped[(k, g)][:, lo * PACK : hi * PACK], rows)
 
         fed = {}
 
@@ -129,7 +143,7 @@ def tile_napl_conv_withsat_pb_t_kernel(tc, supports, cheb_2, spatial_attention, 
             b, g = steps[i]
             fed[i] = []
             if (b, g) in TENSOR_PASSES:
-                rows = map_rows[i][:]
+                rows = rows_in(map_rows[i], 0, NODES)
                 for lo in range(0, NODES, BANK_COLS):
                     bank = map_psum.tile([P, BANK_COLS, 2, 2], BF16)
                     for h in range(2):
@@ -142,9 +156,10 @@ def tile_napl_conv_withsat_pb_t_kernel(tc, supports, cheb_2, spatial_attention, 
                         )
                     fed[i].append((lo, lo + BANK_COLS, bank[:]))
             else:
-                attention = attention_pool.tile([P, 2, NODES, 2], BF16)
-                pair_rows(nc.scalar.copy, attention[:], map_rows[i][:])
-                fed[i].append((0, NODES, attention[:].rearrange("p h w e -> p w h e")))
+                for lo, hi in HALVES if i == 0 else [(0, NODES)]:
+                    attention = attention_pool.tile([P, 2, hi - lo, 2], BF16, tag="attention")
+                    pair_rows(nc.scalar.copy, attention[:], rows_in(map_rows[i], lo, hi))
+                    fed[i].append((lo, hi, attention[:].rearrange("p h w e -> p w h e")))
 
         x_grouped = {}
 
@@ -231,7 +246,7 @@ def tile_napl_conv_withsat_pb_t_kernel(tc, supports, cheb_2, spatial_attention, 
                     :, :, 0 : (PACK - 1) * (DIAG_WINDOW + 1) + 1 : DIAG_WINDOW + 1
                 ],
             )
-            scaled_x = result_pool.tile([P, PASSES * PACK, CHANNELS], F32)
+            scaled_x = scaled_pool.tile([P, PASSES * PACK, CHANNELS], F32)
             for s in range(PASSES * PACK):
                 nc.scalar.activation(
                     out=scaled_x[:, s, :],
@@ -244,61 +259,66 @@ def tile_napl_conv_withsat_pb_t_kernel(tc, supports, cheb_2, spatial_attention, 
                 in_=scaled_x[:].rearrange("p (g j) c -> p g (j c)", g=PASSES),
             )
 
-        load_map(0)
-        load_term(0, 0)
+        map_rows[0] = new_rows()
+        term_rows[(0, 0)] = new_rows()
+        for lo, hi in HALVES:
+            load_columns(map_rows[0], spatial_attention[0], 0, lo, hi)
+            load_columns(term_rows[(0, 0)], terms[0], 0, lo, hi)
         load_term(1, 0)
-        load_term(0, 1)
         load_map(1)
-        load_term(1, 1)
+        load_map(2)
         feed(0)
-        interleave_term(nc.vector.tensor_copy, 0, 0)
-        interleave_term(nc.scalar.copy, 1, 0)
         feed(1)
         new_operands(0)
         products = [new_product(0, NODES) for k in range(TERMS)]
-        multiply(0, 0, products[0], 0, NODES)
-        interleave_term(nc.vector.tensor_copy, 0, 1)
+        for lo, hi in HALVES:
+            interleave_term(nc.vector.tensor_copy, 0, 0, lo, hi, rows_in(term_rows[(0, 0)], lo, hi))
+            multiply(0, 0, products[0], lo, hi)
+        for (lo, hi), copy in zip(HALVES, (nc.vector.tensor_copy, nc.scalar.copy)):
+            interleave_term(copy, 1, 0, lo, hi, rows_in(term_rows[(1, 0)], 0, NODES)[:, :, lo:hi])
+        quantise(0, 0, products[0], 0, NODES)
         multiply(0, 1, products[1], 0, NODES)
-        interleave_term(nc.scalar.copy, 1, 1)
-        load_map(2)
-        load_x(0)
         feed(2)
-        for i in range(3, 6):
-            load_map(i)
-        load_x(1)
         for k in range(TERMS):
-            quantise(0, k, products[k], 0, NODES)
+            load_term(k, 1)
+        load_x(0)
+        load_map(3)
+        load_map(4)
+        load_x(1)
+        load_x(2)
+        quantise(0, 1, products[1], 0, NODES)
 
         waiting = []
         for i in range(1, last_step + 1):
             b, g = steps[i]
+            finishing = sample_finishing.get(i)
             if b not in operands:
                 new_operands(b)
-            if i + 5 <= last_step:
-                load_map(i + 5)
-            if sample_finishing.get(i + 4, 0) >= 2:
+            if i + 4 <= last_step:
+                load_map(i + 4)
+            if sample_finishing.get(i + 4, 0) >= LEADING:
                 load_x(sample_finishing[i + 4])
-            if i == 1:
-                load_diagonal(0)
-            if i + 2 in sample_finishing and sample_finishing[i + 2] > 0:
+            if i + 2 in sample_finishing:
                 load_diagonal(sample_finishing[i + 2])
 
             if i == 1:
-                interleave_x(0)
-            if i + 2 <= last_step:
+                for k in range(TERMS):
+                    interleave_term(nc.scalar.copy, k, 1, 0, NODES, rows_in(term_rows[(k, 1)], 0, NODES))
+            fed_by_tensor = i + 2 <= last_step and steps[i + 2] in TENSOR_PASSES
+            if i + 2 <= last_step and not fed_by_tensor:
                 feed(i + 2)
             for group in waiting:
                 store(*group)
             waiting = []
-            if i == 2:
-                interleave_x(1)
-            if i in (3, 4):
-                scale_x(i - 3)
-            if i == 3 or (i > 4 and i in sample_finishing and i < last_step):
+            if i <= LEADING:
+                interleave_x(i - 1)
+            elif i == 2 * LEADING - 1 or (i > 2 * LEADING and finishing is not None and i < last_step):
                 interleave_x(b + 1)
-            if i > 4 and i in sample_finishing and i < last_step:
+            if LEADING < i <= 2 * LEADING:
+                scale_x(i - LEADING - 1)
+            elif i > 2 * LEADING and finishing is not None and i < last_step:
                 scale_x(b)
-            if i == last_step - 1:
+            elif i == last_step - 1:
                 scale_x(BATCH - 1)
 
             for first, end in column_ranges(i):
@@ -307,11 +327,13 @@ def tile_napl_conv_withsat_pb_t_kernel(tc, supports, cheb_2, spatial_attention, 
                 for lo, hi in pieces:
                     for k in range(TERMS):
                         multiply(i, k, products[k], lo, hi, first)
-                if first == 0 and i in sample_finishing:
+                if fed_by_tensor:
+                    feed(i + 2)
+                if first == 0 and finishing is not None:
                     quantise_x(b)
                 for k in range(TERMS):
                     quantise(i, k, products[k], first, end)
-                if i in sample_finishing:
+                if finishing is not None:
                     for k in range(TERMS):
                         for lo in range(first, end, OUT_COLS):
                             group = contract(b, k, lo, min(lo + OUT_COLS, end))

from contextlib import ExitStack

import concourse.mybir as mybir
from concourse.masks import make_identity

BF16 = mybir.dt.bfloat16
F32 = mybir.dt.float32
U32 = mybir.dt.uint32
U8 = mybir.dt.uint8
FP8X4 = mybir.dt.float8_e4m3fn_x4

P = 128
PACK = 4
K_PASS = P * PACK

BATCH = 8
NODES = 1024
CHANNELS = 128
TERMS = 2
PASSES = NODES // K_PASS
GROUPED = NODES * PACK
RUN = 4
OUT_COLS = 512
BANK_COLS = 256
DIAG_WINDOW = 16
DIAG_STRIDE = PACK * DIAG_WINDOW + DIAG_WINDOW - PACK
LAST_WIDTHS = (512, 256, 128, 128)
TENSOR_PASSES = ((1, 0), (0, 1), (4, 0))

HALVES = ((0, NODES // 2), (NODES // 2, NODES))
LEADING = 3

FLOPS = 2 * TERMS * BATCH * NODES * NODES * CHANNELS


def interleave(copy, grouped, rows):
    copy(
        out=grouped.rearrange("p (c i j) -> p c j i", i=RUN, j=PACK),
        in_=rows.rearrange("p j (c i) -> p c j i", i=RUN),
    )


def pair_rows(copy, paired, rows):
    copy(out=paired, in_=rows.rearrange("p (h e) w -> p h w e", h=2))


def tile_napl_conv_withsat_pb_t_kernel(tc, supports, cheb_2, spatial_attention, x, out):
    nc = tc.nc
    terms = (supports, cheb_2)

    leading = range(LEADING)
    steps = [(b, g) for g in range(PASSES) for b in leading]
    steps += [(b, g) for b in range(LEADING, BATCH) for g in range(PASSES)]
    finish = {b: steps.index((b, PASSES - 1)) for b in range(BATCH)}
    sample_finishing = {step: b for b, step in finish.items()}
    last_step = len(steps) - 1

    with ExitStack() as ctx:
        keep = ctx.enter_context(tc.tile_pool(name="keep", bufs=1))
        rows_pool = ctx.enter_context(tc.tile_pool(name="rows", bufs=5))
        attention_pool = ctx.enter_context(tc.tile_pool(name="attention", bufs=3))
        product_pool = ctx.enter_context(tc.tile_pool(name="product", bufs=4))
        operand_pool = ctx.enter_context(tc.tile_pool(name="operand", bufs=3))
        x_pool = ctx.enter_context(tc.tile_pool(name="x", bufs=4))
        result_pool = ctx.enter_context(tc.tile_pool(name="result", bufs=4))
        scaled_pool = ctx.enter_context(tc.tile_pool(name="scaled", bufs=2))
        psum = ctx.enter_context(tc.psum_pool(name="psum", bufs=4))
        map_psum = ctx.enter_context(tc.psum_pool(name="map", bufs=4))
        identity = keep.tile([P, P], BF16)
        make_identity(nc, identity[:])
        ctx.enter_context(tc.manual_schedule())

        def column_ranges(i):
            if i != last_step:
                return [(0, NODES)]
            starts = [sum(LAST_WIDTHS[:n]) for n in range(len(LAST_WIDTHS))]
            return [(start, start + width) for start, width in zip(starts, LAST_WIDTHS)]

        def new_rows():
            rows = rows_pool.tile([P, GROUPED], BF16, tag="rows")
            return rows

        def rows_in(rows, lo, hi):
            return rows[:, lo * PACK : hi * PACK].rearrange("p (j w) -> p j w", j=PACK)

        def load_columns(rows, matrix, g, lo, hi):
            nc.sync.dma_start(
                out=rows_in(rows, lo, hi),
                in_=matrix[g * K_PASS : (g + 1) * K_PASS, lo:hi].rearrange("(p j) m -> p j m", j=PACK),
            )

        map_rows = {}

        def load_map(i):
            b, g = steps[i]
            map_rows[i] = new_rows()
            load_columns(map_rows[i], spatial_attention[b], g, 0, NODES)

        x_rows = {}

        def load_x(b):
            x_rows[b] = x_pool.tile([P, PASSES * PACK, CHANNELS], BF16, name="x_rows")
            nc.sync.dma_start(
                out=x_rows[b][:].rearrange("p (g j) c -> p g (j c)", g=PASSES),
                in_=x[b].rearrange("(g p j) f t -> p g (j f t)", g=PASSES, j=PACK),
            )

        diag_windows = {}

        def load_diagonal(b):
            window = x_pool.tile([P, PASSES * DIAG_STRIDE], BF16, name="diag_window")
            diag_windows[b] = window
            flat_map = spatial_attention[b].rearrange("n m -> (n m)")
            block = PACK * (NODES + 1)
            for g in range(PASSES):
                if g == 0:
                    half, row_start, first = flat_map[: P * block], 0, 0
                else:
                    half, row_start, first = flat_map[NODES * NODES - P * block :], PACK, NODES - DIAG_WINDOW
                size = PACK * DIAG_WINDOW
                nc.sync.dma_start(
                    out=window[:, g * size : (g + 1) * size].rearrange("p (j c) -> p j c", j=PACK),
                    in_=half.rearrange("(p s) -> p s", p=P)[:, row_start : row_start + PACK * NODES].rearrange(
                        "p (j m) -> p j m", j=PACK
                    )[:, :, first : first + DIAG_WINDOW],
                )

        term_rows = {}
        term_grouped = {}

        def load_term(k, g):
            term_rows[(k, g)] = new_rows()
            load_columns(term_rows[(k, g)], terms[k], g, 0, NODES)

        def interleave_term(copy, k, g, lo, hi, rows):
            if (k, g) not in term_grouped:
                term_grouped[(k, g)] = keep.tile([P, GROUPED], BF16, name="term%d_pass%d" % (k, g))
            interleave(copy, term_grouped[(k, g)][:, lo * PACK : hi * PACK], rows)

        fed = {}

        def feed(i):
            b, g = steps[i]
            fed[i] = []
            if (b, g) in TENSOR_PASSES:
                rows = rows_in(map_rows[i], 0, NODES)
                for lo in range(0, NODES, BANK_COLS):
                    bank = map_psum.tile([P, BANK_COLS, 2, 2], BF16)
                    for h in range(2):
                        nc.tensor.matmul(
                            out=bank[:, :, h, :],
                            lhsT=identity[:],
                            rhs=rows[:, 2 * h : 2 * h + 2, lo : lo + BANK_COLS].rearrange("p e w -> p w e"),
                            start=True,
                            stop=True,
                        )
                    fed[i].append((lo, lo + BANK_COLS, bank[:]))
            else:
                for lo, hi in HALVES if i == 0 else [(0, NODES)]:
                    attention = attention_pool.tile([P, 2, hi - lo, 2], BF16, tag="attention")
                    pair_rows(nc.scalar.copy, attention[:], rows_in(map_rows[i], lo, hi))
                    fed[i].append((lo, hi, attention[:].rearrange("p h w e -> p w h e")))

        x_grouped = {}

        def interleave_x(b):
            x_grouped[b] = x_pool.tile([P, PASSES, CHANNELS * PACK], BF16, align_bytes=64, name="x_grouped")
            for g in range(PASSES):
                interleave(nc.scalar.copy, x_grouped[b][:, g, :], x_rows[b][:, g * PACK : (g + 1) * PACK, :])

        x_operand = {}

        def quantise_x(b):
            x_codes = x_pool.tile([P, PASSES, CHANNELS], U32, align_bytes=64)
            x_scales = x_pool.tile([P, PASSES, CHANNELS], U8, align_bytes=64)
            nc.vector.quantize_mx(
                out=x_codes[:].rearrange("p g c -> p (g c)").bitcast(FP8X4),
                scales=x_scales[:].rearrange("p g c -> p (g c)"),
                in_=x_grouped[b][:].rearrange("p g v -> p (g v)"),
            )
            x_operand[b] = (x_codes, x_scales)

        operands = {}

        def new_operands(b):
            operands[b] = []
            for k in range(TERMS):
                codes = operand_pool.tile([P, PASSES, NODES], U32, align_bytes=64, name="w_codes%d" % k)
                scales = operand_pool.tile([P, PASSES, NODES], U8, align_bytes=64, name="w_scales%d" % k)
                operands[b].append((codes, scales))

        def new_product(lo, hi):
            product = product_pool.tile([P, (hi - lo) * PACK], BF16, align_bytes=64, tag="product")
            return product

        def multiply(i, k, product, lo, hi, start=0):
            for fed_lo, fed_hi, map_columns in fed[i]:
                first, end = max(lo, fed_lo), min(hi, fed_hi)
                if first < end:
                    span = slice(first * PACK, end * PACK)
                    here = slice((first - start) * PACK, (end - start) * PACK)
                    nc.vector.tensor_tensor(
                        out=product[:, here].rearrange("p (w h e) -> p w h e", h=2, e=2),
                        in0=term_grouped[(k, steps[i][1])][:, span].rearrange("p (w h e) -> p w h e", h=2, e=2),
                        in1=map_columns[:, first - fed_lo : end - fed_lo, :, :],
                        op=mybir.AluOpType.mult,
                    )

        def quantise(i, k, product, lo, hi):
            b, g = steps[i]
            codes, scales = operands[b][k]
            nc.vector.quantize_mx(
                out=codes[:, g, lo:hi].bitcast(FP8X4), scales=scales[:, g, lo:hi], in_=product[:]
            )

        def contract(b, k, lo, hi):
            codes, scales = operands[b][k]
            x_codes, x_scales = x_operand[b]
            acc = psum.tile([P, (hi - lo) // P, CHANNELS], F32, tag="acc")
            for t in range((hi - lo) // P):
                m_cols = slice(lo + t * P, lo + (t + 1) * P)
                for g in range(PASSES):
                    nc.tensor.matmul_mx(
                        out=acc[:, t, :],
                        lhsT=codes[:, g, m_cols].bitcast(FP8X4),
                        lhsT_scale=scales[:, g, m_cols],
                        rhs=x_codes[:, g, :].bitcast(FP8X4),
                        rhs_scale=x_scales[:, g, :],
                        start=(g == 0),
                        stop=(g == PASSES - 1),
                    )
            return b, k, lo, hi, acc

        def store(b, k, lo, hi, acc):
            result = result_pool.tile([P, (hi - lo) // P, CHANNELS], F32, tag="result")
            nc.scalar.copy(out=result[:], in_=acc[:])
            nc.sync.dma_start(
                out=out[1 + k, b, lo:hi].rearrange("(t q) f s -> q t (f s)", q=P), in_=result[:]
            )

        def scale_x(b):
            diag = x_pool.tile([P, PASSES * PACK], F32)
            nc.scalar.copy(
                out=diag[:].rearrange("p (g j) -> p g j", g=PASSES),
                in_=diag_windows[b][:].rearrange("p (g s) -> p g s", g=PASSES)[
                    :, :, 0 : (PACK - 1) * (DIAG_WINDOW + 1) + 1 : DIAG_WINDOW + 1
                ],
            )
            scaled_x = scaled_pool.tile([P, PASSES * PACK, CHANNELS], F32)
            for s in range(PASSES * PACK):
                nc.scalar.activation(
                    out=scaled_x[:, s, :],
                    in_=x_rows[b][:, s, :],
                    func=mybir.ActivationFunctionType.Copy,
                    scale=diag[:, s : s + 1],
                )
            nc.sync.dma_start(
                out=out[0, b].rearrange("(g p j) f t -> p g (j f t)", g=PASSES, j=PACK),
                in_=scaled_x[:].rearrange("p (g j) c -> p g (j c)", g=PASSES),
            )

        map_rows[0] = new_rows()
        term_rows[(0, 0)] = new_rows()
        for lo, hi in HALVES:
            load_columns(map_rows[0], spatial_attention[0], 0, lo, hi)
            load_columns(term_rows[(0, 0)], terms[0], 0, lo, hi)
        load_term(1, 0)
        load_map(1)
        load_map(2)
        feed(0)
        feed(1)
        new_operands(0)
        products = [new_product(0, NODES) for k in range(TERMS)]
        for lo, hi in HALVES:
            interleave_term(nc.vector.tensor_copy, 0, 0, lo, hi, rows_in(term_rows[(0, 0)], lo, hi))
            multiply(0, 0, products[0], lo, hi)
        for (lo, hi), copy in zip(HALVES, (nc.vector.tensor_copy, nc.scalar.copy)):
            interleave_term(copy, 1, 0, lo, hi, rows_in(term_rows[(1, 0)], 0, NODES)[:, :, lo:hi])
        quantise(0, 0, products[0], 0, NODES)
        multiply(0, 1, products[1], 0, NODES)
        feed(2)
        for k in range(TERMS):
            load_term(k, 1)
        load_x(0)
        load_map(3)
        load_map(4)
        load_x(1)
        load_x(2)
        quantise(0, 1, products[1], 0, NODES)

        waiting = []
        for i in range(1, last_step + 1):
            b, g = steps[i]
            finishing = sample_finishing.get(i)
            if b not in operands:
                new_operands(b)
            if i + 4 <= last_step:
                load_map(i + 4)
            if sample_finishing.get(i + 4, 0) >= LEADING:
                load_x(sample_finishing[i + 4])
            if i + 2 in sample_finishing:
                load_diagonal(sample_finishing[i + 2])

            if i == 1:
                for k in range(TERMS):
                    interleave_term(nc.scalar.copy, k, 1, 0, NODES, rows_in(term_rows[(k, 1)], 0, NODES))
            fed_by_tensor = i + 2 <= last_step and steps[i + 2] in TENSOR_PASSES
            if i + 2 <= last_step and not fed_by_tensor:
                feed(i + 2)
            for group in waiting:
                store(*group)
            waiting = []
            if i <= LEADING:
                interleave_x(i - 1)
            elif i == 2 * LEADING - 1 or (i > 2 * LEADING and finishing is not None and i < last_step):
                interleave_x(b + 1)
            if LEADING < i <= 2 * LEADING:
                scale_x(i - LEADING - 1)
            elif i > 2 * LEADING and finishing is not None and i < last_step:
                scale_x(b)
            elif i == last_step - 1:
                scale_x(BATCH - 1)

            for first, end in column_ranges(i):
                products = [new_product(first, end) for k in range(TERMS)]
                pieces = [(max(first, lo), min(end, hi)) for lo, hi, columns in fed[i]]
                for lo, hi in pieces:
                    for k in range(TERMS):
                        multiply(i, k, products[k], lo, hi, first)
                if fed_by_tensor:
                    feed(i + 2)
                if first == 0 and finishing is not None:
                    quantise_x(b)
                for k in range(TERMS):
                    quantise(i, k, products[k], first, end)
                if finishing is not None:
                    for k in range(TERMS):
                        for lo in range(first, end, OUT_COLS):
                            group = contract(b, k, lo, min(lo + OUT_COLS, end))
                            if i == last_step:
                                store(*group)
                            else:
                                waiting.append(group)
